import numpy as np
import ml_dtypes

BF16 = ml_dtypes.bfloat16


def bf(x):
    return np.asarray(x, np.float32).astype(BF16)


def f32(x):
    return np.asarray(x, np.float32)


def f64(x):
    return np.asarray(x).astype(np.float64)


def striped(idx):
    return np.tile(idx.reshape(-1, 16).T, (8, 1))


C, S, N, K, H = 128, 4096, 1024, 16, 4
DH = C // H


def setup_inputs():
    return {"f": f32(np.random.standard_normal((C, S))), "nb": f32(np.random.standard_normal((C, K, N))), "w_q": bf(np.random.standard_normal((C, C)) / np.sqrt(C)), "b_q": f32(0.1 * np.random.standard_normal((C, 1))), "b_o": f32(0.1 * np.random.standard_normal((C, 1))), "offs": striped(np.random.permutation(S)[:N])}


def reference(f, nb, w_q, b_q, b_o, offs):
    idx = offs[:16].T.reshape(-1)
    fn = f64(f)[:, idx]
    q = f64(w_q).T @ fn + f64(b_q)
    nbr = f64(nb).reshape(H, DH, K, N)
    score = (q.reshape(H, DH, N)[:, :, None, :] * nbr).sum(axis=1) / np.sqrt(DH)
    e = np.exp(score - score.max(axis=1, keepdims=True))
    attn = e / e.sum(axis=1, keepdims=True)
    o = (attn[:, None, :, :] * nbr).sum(axis=2).reshape(C, N)
    return fn + o + f64(b_o)

@@ -1,0 +1,162 @@
+import math
+
+import concourse.mybir as mybir
+from concourse.masks import make_identity
+
+F32, BF16, U16 = mybir.dt.float32, mybir.dt.bfloat16, mybir.dt.uint16
+ALU = mybir.AluOpType
+ACT = mybir.ActivationFunctionType
+
+C, S, N, T, H = 128, 4096, 1024, 16, 4
+DH = C // H
+SCALE = 1.0 / math.sqrt(DH)
+
+BLOCK = 128
+CHUNK = 256
+NCHUNK = N // CHUNK
+NBLOCK = CHUNK // BLOCK
+G, U = 2, 8
+PIECES = 3
+ROWS = PIECES * H * U
+
+FLOPS = 2 * C * C * N + 2 * 2 * C * T * N
+
+
+def tile_localppftransformer_kernel(tc, f, nb, w_q, b_q, b_o, offs, out):
+    nc = tc.nc
+    with (
+        tc.tile_pool(name="held", bufs=1) as held,
+        tc.tile_pool(name="neighbours", bufs=NCHUNK) as neighbours,
+        tc.tile_pool(name="work", bufs=2) as work,
+        tc.psum_pool(name="psum_q", bufs=1) as psum_q,
+        tc.psum_pool(name="psum_one", bufs=1) as psum_one,
+        tc.psum_pool(name="psum_spread", bufs=3) as psum_spread,
+    ):
+        offsets = held.tile([C, N // 16], U16, name="offsets")
+        nc.sync.dma_start(offsets[:], offs)
+        table = held.tile([C, S], F32, name="table")
+        nc.sync.dma_start(table[:], f)
+        wq = held.tile([C, C], BF16, name="wq")
+        nc.scalar.dma_start(wq[:], w_q)
+        bq = held.tile([C, 1], F32, name="bq")
+        nc.scalar.dma_start(bq[:], b_q)
+        bo = held.tile([C, 1], F32, name="bo")
+        nc.scalar.dma_start(bo[:], b_o)
+
+        head_of = held.tile([C, H], BF16, name="head_of")
+        nc.gpsimd.memset(head_of[:], 0.0)
+        for h in range(H):
+            nc.gpsimd.memset(head_of[h * DH : (h + 1) * DH, h : h + 1], 1.0)
+        ident_bf = held.tile([C, C], BF16, name="ident_bf")
+        make_identity(nc, ident_bf[:])
+        ident_f = held.tile([C, C], F32, name="ident_f")
+        make_identity(nc, ident_f[:])
+        spread = held.tile([ROWS, U, H, DH], BF16, name="spread")
+        nc.gpsimd.memset(spread[:], 0.0)
+        for piece in range(PIECES):
+            nc.gpsimd.affine_select(
+                out=spread[:], in_=spread[:], compare_op=ALU.not_equal, fill=1.0,
+                base=-H * U * piece, channel_multiplier=1, pattern=[[-1, U], [-U, H], [0, DH]],
+            )
+
+        fn = held.tile([C, N], F32, name="fn")
+        nc.scalar.activation(fn[:], table[:].indirect(offsets[:]), ACT.Copy)
+        fn_bf = held.tile([C, N], BF16, name="fn_bf")
+        nc.vector.tensor_copy(fn_bf[:], fn[:])
+        residual = held.tile([C, N], F32, name="residual")
+        nc.scalar.activation(residual[:], fn[:], ACT.Identity, bias=bo[:, 0:1])
+        q_banks = []
+        for k in range(N // 512):
+            q_bank = psum_q.tile([C, 512], F32, name=f"q_bank{k}")
+            nc.tensor.matmul(q_bank[:], wq[:], fn_bf[:, k * 512 : (k + 1) * 512])
+            q_banks.append(q_bank)
+
+        for i in range(NCHUNK):
+            j0 = i * CHUNK
+            nbr = neighbours.tile([C, T, CHUNK], F32, name="nbr")
+            nc.sync.dma_start(nbr[:], nb[:, :, j0 : j0 + CHUNK])
+            q_chunk = q_banks[j0 // 512][:, j0 % 512 : j0 % 512 + CHUNK]
+
+            prod = work.tile([C, T, CHUNK], BF16, name="prod")
+            for g in range(G):
+                nc.vector.scalar_tensor_tensor(
+                    out=prod[:, g * U : (g + 1) * U, :],
+                    in0=q_chunk.unsqueeze(1).to_broadcast([C, U, CHUNK]),
+                    scalar=bq[:, 0:1],
+                    in1=nbr[:, g * U : (g + 1) * U, :],
+                    op0=ALU.add, op1=ALU.mult,
+                )
+
+            score = psum_one.tile([BLOCK, NBLOCK, G, H, U], F32, name="score")
+            for b in range(NBLOCK):
+                for g in range(G):
+                    for u in range(U):
+                        nc.tensor.matmul(
+                            score[:, b, g, :, u],
+                            prod[:, g * U + u, b * BLOCK : (b + 1) * BLOCK],
+                            head_of[:],
+                        )
+
+            neg_max = work.tile([BLOCK, NBLOCK, H], F32, name="neg_max")
+            nc.vector.tensor_reduce(
+                out=neg_max[:], in_=score[:].rearrange("p b g h u -> p b h g u"),
+                axis=mybir.AxisListType.XY, op=ALU.max, negate=True,
+            )
+            shift = work.tile([BLOCK, NBLOCK, H], F32, name="shift")
+            nc.scalar.mul(shift[:], neg_max[:], SCALE)
+            expo = work.tile([BLOCK, NBLOCK, G, H, U], F32, name="expo")
+            total = work.tile([BLOCK, NBLOCK, H], F32, name="total")
+            for b in range(NBLOCK):
+                for h in range(H):
+                    nc.scalar.activation(
+                        expo[:, b, :, h, :], score[:, b, :, h, :], ACT.Exp,
+                        bias=shift[:, b, h : h + 1], scale=SCALE, accum_out=total[:, b, h : h + 1],
+                    )
+            inverse = work.tile([BLOCK, NBLOCK, H], F32, name="inverse")
+            nc.vector.reciprocal(inverse[:], total[:])
+            attn = work.tile([BLOCK, NBLOCK, G, H, U], F32, name="attn")
+            for b in range(NBLOCK):
+                for h in range(H):
+                    nc.scalar.activation(
+                        attn[:, b, :, h, :], expo[:, b, :, h, :], ACT.Copy, scale=inverse[:, b, h : h + 1],
+                    )
+
+            attn_flat = attn[:].rearrange("p b g h u -> p (b g) (h u)")
+            pieces = work.tile([BLOCK, NBLOCK * G, PIECES, H * U], BF16, name="pieces")
+            rest = work.tile([BLOCK, NBLOCK * G, H * U], F32, name="rest")
+            nc.vector.tensor_copy(pieces[:, :, 0, :], attn_flat)
+            nc.vector.tensor_tensor(rest[:], attn_flat, pieces[:, :, 0, :], ALU.subtract)
+            nc.vector.tensor_copy(pieces[:, :, 1, :], rest[:])
+            nc.vector.tensor_tensor(pieces[:, :, 2, :], rest[:], pieces[:, :, 1, :], ALU.subtract)
+
+            flipped_ps = psum_one.tile([ROWS, G, CHUNK], BF16, name="flipped_ps")
+            for b in range(NBLOCK):
+                for g in range(G):
+                    nc.tensor.transpose(
+                        flipped_ps[:, g, b * BLOCK : (b + 1) * BLOCK],
+                        pieces[:, b * G + g, :, :].rearrange("p k x -> p (k x)"),
+                        ident_bf[:],
+                    )
+            flipped = work.tile([ROWS, G, CHUNK], BF16, name="flipped")
+            nc.scalar.copy(flipped[:], flipped_ps[:])
+
+            weighted = work.tile([C, T, CHUNK], F32, name="weighted")
+            for t in range(0, T, 2):
+                attn_c = psum_spread.tile([C, 2, CHUNK], F32, name="attn_c")
+                for k in range(2):
+                    nc.tensor.matmul(
+                        attn_c[:, k, :],
+                        spread[:, (t + k) % U, :, :].rearrange("r h d -> r (h d)"),
+                        flipped[:, (t + k) // U, :],
+                    )
+                nc.vector.tensor_tensor(weighted[:, t : t + 2, :], attn_c[:], nbr[:, t : t + 2, :], ALU.mult)
+
+            halves = work.tile([C, U, CHUNK], F32, name="halves")
+            nc.gpsimd.tensor_tensor(halves[:], weighted[:, 0:U, :], weighted[:, U:T, :], ALU.add)
+            o_ps = psum_one.tile([C, CHUNK], F32, name="o_ps")
+            for u in range(U):
+                nc.tensor.matmul(o_ps[:], ident_f[:], halves[:, u, :], start=(u == 0), stop=(u == U - 1))
+
+            result = work.tile([C, CHUNK], F32, name="result")
+            nc.vector.tensor_tensor(result[:], o_ps[:], residual[:, j0 : j0 + CHUNK], ALU.add)
+            nc.sync.dma_start(out[:, j0 : j0 + CHUNK], result[:])

@@ -11,6 +11,7 @@ C, S, N, T, H = 128, 4096, 1024, 16, 4
 DH = C // H
 SCALE = 1.0 / math.sqrt(DH)
 
+BANK = 512
 BLOCK = 128
 CHUNK = 256
 NCHUNK = N // CHUNK
@@ -18,6 +19,7 @@ NBLOCK = CHUNK // BLOCK
 G, U = 2, 8
 PIECES = 3
 ROWS = PIECES * H * U
+T_POOL = 7
 
 FLOPS = 2 * C * C * N + 2 * 2 * C * T * N
 
@@ -26,16 +28,20 @@ def tile_localppftransformer_kernel(tc, f, nb, w_q, b_q, b_o, offs, out):
     nc = tc.nc
     with (
         tc.tile_pool(name="held", bufs=1) as held,
-        tc.tile_pool(name="neighbours", bufs=NCHUNK) as neighbours,
         tc.tile_pool(name="work", bufs=2) as work,
-        tc.psum_pool(name="psum_q", bufs=1) as psum_q,
-        tc.psum_pool(name="psum_one", bufs=1) as psum_one,
-        tc.psum_pool(name="psum_spread", bufs=3) as psum_spread,
+        tc.psum_pool(name="psum_held", bufs=1) as psum_held,
+        tc.psum_pool(name="psum_ring", bufs=4) as psum_ring,
     ):
         offsets = held.tile([C, N // 16], U16, name="offsets")
         nc.sync.dma_start(offsets[:], offs)
         table = held.tile([C, S], F32, name="table")
         nc.sync.dma_start(table[:], f)
+        nbr = [held.tile([C, T, CHUNK], F32, name=f"nbr{i}") for i in range(NCHUNK)]
+        for i in range(NCHUNK):
+            for g in range(G):
+                nc.sync.dma_start(
+                    nbr[i][:, g * U : (g + 1) * U, :], nb[:, g * U : (g + 1) * U, i * CHUNK : (i + 1) * CHUNK]
+                )
         wq = held.tile([C, C], BF16, name="wq")
         nc.scalar.dma_start(wq[:], w_q)
         bq = held.tile([C, 1], F32, name="bq")
@@ -43,14 +49,15 @@ def tile_localppftransformer_kernel(tc, f, nb, w_q, b_q, b_o, offs, out):
         bo = held.tile([C, 1], F32, name="bo")
         nc.scalar.dma_start(bo[:], b_o)
 
+        warm = held.tile([C, 1], F32, name="warm")
+        nc.vector.memset(warm[:], 0.0)
+        nc.scalar.activation(warm[:], warm[:], ACT.Exp)
         head_of = held.tile([C, H], BF16, name="head_of")
         nc.gpsimd.memset(head_of[:], 0.0)
         for h in range(H):
             nc.gpsimd.memset(head_of[h * DH : (h + 1) * DH, h : h + 1], 1.0)
-        ident_bf = held.tile([C, C], BF16, name="ident_bf")
-        make_identity(nc, ident_bf[:])
-        ident_f = held.tile([C, C], F32, name="ident_f")
-        make_identity(nc, ident_f[:])
+        identity = held.tile([C, C], BF16, name="identity")
+        make_identity(nc, identity[:])
         spread = held.tile([ROWS, U, H, DH], BF16, name="spread")
         nc.gpsimd.memset(spread[:], 0.0)
         for piece in range(PIECES):
@@ -60,41 +67,46 @@ def tile_localppftransformer_kernel(tc, f, nb, w_q, b_q, b_o, offs, out):
             )
 
         fn = held.tile([C, N], F32, name="fn")
-        nc.scalar.activation(fn[:], table[:].indirect(offsets[:]), ACT.Copy)
         fn_bf = held.tile([C, N], BF16, name="fn_bf")
-        nc.vector.tensor_copy(fn_bf[:], fn[:])
+        q_sbuf = held.tile([C, N], F32, name="q_sbuf")
         residual = held.tile([C, N], F32, name="residual")
+        q_psum = []
+        for k in range(N // BANK):
+            piece_of_list = offsets[:, k * (BANK // 16) : (k + 1) * (BANK // 16)]
+            columns = slice(k * BANK, (k + 1) * BANK)
+            nc.scalar.activation(fn[:, columns], table[:].indirect(piece_of_list), ACT.Copy)
+            nc.vector.tensor_copy(fn_bf[:, columns], fn[:, columns])
+            q_bank = psum_held.tile([C, BANK], F32, name=f"q_bank{k}")
+            nc.tensor.matmul(q_bank[:], wq[:], fn_bf[:, columns])
+            q_psum.append(q_bank)
+            nc.scalar.activation(q_sbuf[:, columns], q_bank[:], ACT.Identity, bias=bq[:, 0:1])
         nc.scalar.activation(residual[:], fn[:], ACT.Identity, bias=bo[:, 0:1])
-        q_banks = []
-        for k in range(N // 512):
-            q_bank = psum_q.tile([C, 512], F32, name=f"q_bank{k}")
-            nc.tensor.matmul(q_bank[:], wq[:], fn_bf[:, k * 512 : (k + 1) * 512])
-            q_banks.append(q_bank)
 
+        flipped = []
         for i in range(NCHUNK):
             j0 = i * CHUNK
-            nbr = neighbours.tile([C, T, CHUNK], F32, name="nbr")
-            nc.sync.dma_start(nbr[:], nb[:, :, j0 : j0 + CHUNK])
-            q_chunk = q_banks[j0 // 512][:, j0 % 512 : j0 % 512 + CHUNK]
 
             prod = work.tile([C, T, CHUNK], BF16, name="prod")
-            for g in range(G):
-                nc.vector.scalar_tensor_tensor(
-                    out=prod[:, g * U : (g + 1) * U, :],
-                    in0=q_chunk.unsqueeze(1).to_broadcast([C, U, CHUNK]),
-                    scalar=bq[:, 0:1],
-                    in1=nbr[:, g * U : (g + 1) * U, :],
-                    op0=ALU.add, op1=ALU.mult,
-                )
+            nc.gpsimd.tensor_tensor(
+                prod[:, 0:T_POOL, :],
+                q_sbuf[:, j0 : j0 + CHUNK].unsqueeze(1).to_broadcast([C, T_POOL, CHUNK]),
+                nbr[i][:, 0:T_POOL, :],
+                ALU.mult,
+            )
+            nc.vector.scalar_tensor_tensor(
+                out=prod[:, T_POOL:T, :],
+                in0=q_psum[j0 // BANK][:, j0 % BANK : j0 % BANK + CHUNK].unsqueeze(1).to_broadcast([C, T - T_POOL, CHUNK]),
+                scalar=bq[:, 0:1],
+                in1=nbr[i][:, T_POOL:T, :],
+                op0=ALU.add, op1=ALU.mult,
+            )
 
-            score = psum_one.tile([BLOCK, NBLOCK, G, H, U], F32, name="score")
-            for b in range(NBLOCK):
-                for g in range(G):
-                    for u in range(U):
+            score = psum_held.tile([BLOCK, NBLOCK, G, H, U], F32, name="score")
+            for g in range(G):
+                for u in range(U):
+                    for b in range(NBLOCK):
                         nc.tensor.matmul(
-                            score[:, b, g, :, u],
-                            prod[:, g * U + u, b * BLOCK : (b + 1) * BLOCK],
-                            head_of[:],
+                            score[:, b, g, :, u], prod[:, g * U + u, b * BLOCK : (b + 1) * BLOCK], head_of[:]
                         )
 
             neg_max = work.tile([BLOCK, NBLOCK, H], F32, name="neg_max")
@@ -116,10 +128,10 @@ def tile_localppftransformer_kernel(tc, f, nb, w_q, b_q, b_o, offs, out):
             nc.vector.reciprocal(inverse[:], total[:])
             attn = work.tile([BLOCK, NBLOCK, G, H, U], F32, name="attn")
             for b in range(NBLOCK):
-                for h in range(H):
-                    nc.scalar.activation(
-                        attn[:, b, :, h, :], expo[:, b, :, h, :], ACT.Copy, scale=inverse[:, b, h : h + 1],
-                    )
+                nc.vector.tensor_tensor(
+                    attn[:, b], expo[:, b],
+                    inverse[:, b, :].unsqueeze(1).unsqueeze(3).to_broadcast([BLOCK, G, H, U]), ALU.mult,
+                )
 
             attn_flat = attn[:].rearrange("p b g h u -> p (b g) (h u)")
             pieces = work.tile([BLOCK, NBLOCK * G, PIECES, H * U], BF16, name="pieces")
@@ -129,34 +141,42 @@ def tile_localppftransformer_kernel(tc, f, nb, w_q, b_q, b_o, offs, out):
             nc.vector.tensor_copy(pieces[:, :, 1, :], rest[:])
             nc.vector.tensor_tensor(pieces[:, :, 2, :], rest[:], pieces[:, :, 1, :], ALU.subtract)
 
-            flipped_ps = psum_one.tile([ROWS, G, CHUNK], BF16, name="flipped_ps")
+            flipped_ps = psum_held.tile([ROWS, G, CHUNK], BF16, name="flipped_ps")
             for b in range(NBLOCK):
                 for g in range(G):
                     nc.tensor.transpose(
                         flipped_ps[:, g, b * BLOCK : (b + 1) * BLOCK],
                         pieces[:, b * G + g, :, :].rearrange("p k x -> p (k x)"),
-                        ident_bf[:],
+                        identity[:],
                     )
-            flipped = work.tile([ROWS, G, CHUNK], BF16, name="flipped")
-            nc.scalar.copy(flipped[:], flipped_ps[:])
+            flipped.append(held.tile([ROWS, G, CHUNK], BF16, name=f"flipped{i}"))
+            nc.scalar.copy(flipped[i][:], flipped_ps[:])
 
-            weighted = work.tile([C, T, CHUNK], F32, name="weighted")
-            for t in range(0, T, 2):
-                attn_c = psum_spread.tile([C, 2, CHUNK], F32, name="attn_c")
-                for k in range(2):
-                    nc.tensor.matmul(
-                        attn_c[:, k, :],
-                        spread[:, (t + k) % U, :, :].rearrange("r h d -> r (h d)"),
-                        flipped[:, (t + k) // U, :],
-                    )
-                nc.vector.tensor_tensor(weighted[:, t : t + 2, :], attn_c[:], nbr[:, t : t + 2, :], ALU.mult)
+        def sum_of_eight(engine, eight, who):
+            four = work.tile([C, 4, CHUNK], F32, name="four_" + who)
+            engine.tensor_tensor(four[:], eight[:, :, 0, :], eight[:, :, 1, :], ALU.add)
+            two = work.tile([C, 2, CHUNK], F32, name="two_" + who)
+            engine.tensor_tensor(two[:], four[:, 0:2, :], four[:, 2:4, :], ALU.add)
+            one = work.tile([C, CHUNK], F32, name="one_" + who)
+            engine.tensor_tensor(one[:], two[:, 0, :], two[:, 1, :], ALU.add)
+            return one
 
-            halves = work.tile([C, U, CHUNK], F32, name="halves")
-            nc.gpsimd.tensor_tensor(halves[:], weighted[:, 0:U, :], weighted[:, U:T, :], ALU.add)
-            o_ps = psum_one.tile([C, CHUNK], F32, name="o_ps")
+        for i in range(NCHUNK):
+            j0 = i * CHUNK
+            weighted = work.tile([C, U, G, CHUNK], F32, name="weighted")
             for u in range(U):
-                nc.tensor.matmul(o_ps[:], ident_f[:], halves[:, u, :], start=(u == 0), stop=(u == U - 1))
-
+                attn_c = psum_ring.tile([C, G, CHUNK], F32, name="attn_c")
+                for g in range(G):
+                    nc.tensor.matmul(
+                        attn_c[:, g, :], spread[:, u, :, :].rearrange("r h d -> r (h d)"), flipped[i][:, g, :]
+                    )
+                nc.vector.tensor_tensor(
+                    weighted[:, u], attn_c[:], nbr[i][:].rearrange("c (g u) j -> c u g j", g=G)[:, u], ALU.mult
+                )
+            early = sum_of_eight(nc.gpsimd, weighted[:, 0:4], "pool")
+            early_res = work.tile([C, CHUNK], F32, name="early_res")
+            nc.gpsimd.tensor_tensor(early_res[:], early[:], residual[:, j0 : j0 + CHUNK], ALU.add)
+            late = sum_of_eight(nc.vector, weighted[:, 4:8], "vector")
             result = work.tile([C, CHUNK], F32, name="result")
-            nc.vector.tensor_tensor(result[:], o_ps[:], residual[:, j0 : j0 + CHUNK], ALU.add)
+            nc.vector.tensor_tensor(result[:], early_res[:], late[:], ALU.add)
             nc.sync.dma_start(out[:, j0 : j0 + CHUNK], result[:])

@@ -19,7 +19,7 @@ NBLOCK = CHUNK // BLOCK
 G, U = 2, 8
 PIECES = 3
 ROWS = PIECES * H * U
-T_POOL = 7
+T_POOL = 4
 
 FLOPS = 2 * C * C * N + 2 * 2 * C * T * N
 
@@ -30,7 +30,7 @@ def tile_localppftransformer_kernel(tc, f, nb, w_q, b_q, b_o, offs, out):
         tc.tile_pool(name="held", bufs=1) as held,
         tc.tile_pool(name="work", bufs=2) as work,
         tc.psum_pool(name="psum_held", bufs=1) as psum_held,
-        tc.psum_pool(name="psum_ring", bufs=4) as psum_ring,
+        tc.psum_pool(name="psum_ring", bufs=3) as psum_ring,
     ):
         offsets = held.tile([C, N // 16], U16, name="offsets")
         nc.sync.dma_start(offsets[:], offs)
@@ -58,6 +58,8 @@ def tile_localppftransformer_kernel(tc, f, nb, w_q, b_q, b_o, offs, out):
             nc.gpsimd.memset(head_of[h * DH : (h + 1) * DH, h : h + 1], 1.0)
         identity = held.tile([C, C], BF16, name="identity")
         make_identity(nc, identity[:])
+        identity_f = held.tile([C, C], F32, name="identity_f")
+        make_identity(nc, identity_f[:])
         spread = held.tile([ROWS, U, H, DH], BF16, name="spread")
         nc.gpsimd.memset(spread[:], 0.0)
         for piece in range(PIECES):
@@ -75,7 +77,7 @@ def tile_localppftransformer_kernel(tc, f, nb, w_q, b_q, b_o, offs, out):
             piece_of_list = offsets[:, k * (BANK // 16) : (k + 1) * (BANK // 16)]
             columns = slice(k * BANK, (k + 1) * BANK)
             nc.scalar.activation(fn[:, columns], table[:].indirect(piece_of_list), ACT.Copy)
-            nc.vector.tensor_copy(fn_bf[:, columns], fn[:, columns])
+            nc.scalar.copy(fn_bf[:, columns], fn[:, columns])
             q_bank = psum_held.tile([C, BANK], F32, name=f"q_bank{k}")
             nc.tensor.matmul(q_bank[:], wq[:], fn_bf[:, columns])
             q_psum.append(q_bank)
@@ -83,7 +85,8 @@ def tile_localppftransformer_kernel(tc, f, nb, w_q, b_q, b_o, offs, out):
         nc.scalar.activation(residual[:], fn[:], ACT.Identity, bias=bo[:, 0:1])
 
         flipped = []
-        for i in range(NCHUNK):
+
+        def weights_of(i):
             j0 = i * CHUNK
 
             prod = work.tile([C, T, CHUNK], BF16, name="prod")
@@ -93,13 +96,14 @@ def tile_localppftransformer_kernel(tc, f, nb, w_q, b_q, b_o, offs, out):
                 nbr[i][:, 0:T_POOL, :],
                 ALU.mult,
             )
-            nc.vector.scalar_tensor_tensor(
-                out=prod[:, T_POOL:T, :],
-                in0=q_psum[j0 // BANK][:, j0 % BANK : j0 % BANK + CHUNK].unsqueeze(1).to_broadcast([C, T - T_POOL, CHUNK]),
-                scalar=bq[:, 0:1],
-                in1=nbr[i][:, T_POOL:T, :],
-                op0=ALU.add, op1=ALU.mult,
-            )
+            for lo, hi in ((T_POOL, U), (U, T)):
+                nc.vector.scalar_tensor_tensor(
+                    out=prod[:, lo:hi, :],
+                    in0=q_psum[j0 // BANK][:, j0 % BANK : j0 % BANK + CHUNK].unsqueeze(1).to_broadcast([C, hi - lo, CHUNK]),
+                    scalar=bq[:, 0:1],
+                    in1=nbr[i][:, lo:hi, :],
+                    op0=ALU.add, op1=ALU.mult,
+                )
 
             score = psum_held.tile([BLOCK, NBLOCK, G, H, U], F32, name="score")
             for g in range(G):
@@ -128,18 +132,18 @@ def tile_localppftransformer_kernel(tc, f, nb, w_q, b_q, b_o, offs, out):
             nc.vector.reciprocal(inverse[:], total[:])
             attn = work.tile([BLOCK, NBLOCK, G, H, U], F32, name="attn")
             for b in range(NBLOCK):
-                nc.vector.tensor_tensor(
-                    attn[:, b], expo[:, b],
-                    inverse[:, b, :].unsqueeze(1).unsqueeze(3).to_broadcast([BLOCK, G, H, U]), ALU.mult,
-                )
+                for h in range(H):
+                    nc.scalar.activation(
+                        attn[:, b, :, h, :], expo[:, b, :, h, :], ACT.Copy, scale=inverse[:, b, h : h + 1]
+                    )
 
             attn_flat = attn[:].rearrange("p b g h u -> p (b g) (h u)")
             pieces = work.tile([BLOCK, NBLOCK * G, PIECES, H * U], BF16, name="pieces")
             rest = work.tile([BLOCK, NBLOCK * G, H * U], F32, name="rest")
-            nc.vector.tensor_copy(pieces[:, :, 0, :], attn_flat)
-            nc.vector.tensor_tensor(rest[:], attn_flat, pieces[:, :, 0, :], ALU.subtract)
-            nc.vector.tensor_copy(pieces[:, :, 1, :], rest[:])
-            nc.vector.tensor_tensor(pieces[:, :, 2, :], rest[:], pieces[:, :, 1, :], ALU.subtract)
+            nc.scalar.copy(pieces[:, :, 0, :], attn_flat)
+            nc.gpsimd.tensor_tensor(rest[:], attn_flat, pieces[:, :, 0, :], ALU.subtract)
+            nc.gpsimd.tensor_copy(pieces[:, :, 1, :], rest[:])
+            nc.gpsimd.tensor_tensor(pieces[:, :, 2, :], rest[:], pieces[:, :, 1, :], ALU.subtract)
 
             flipped_ps = psum_held.tile([ROWS, G, CHUNK], BF16, name="flipped_ps")
             for b in range(NBLOCK):
@@ -152,31 +156,38 @@ def tile_localppftransformer_kernel(tc, f, nb, w_q, b_q, b_o, offs, out):
             flipped.append(held.tile([ROWS, G, CHUNK], BF16, name=f"flipped{i}"))
             nc.scalar.copy(flipped[i][:], flipped_ps[:])
 
-        def sum_of_eight(engine, eight, who):
-            four = work.tile([C, 4, CHUNK], F32, name="four_" + who)
-            engine.tensor_tensor(four[:], eight[:, :, 0, :], eight[:, :, 1, :], ALU.add)
-            two = work.tile([C, 2, CHUNK], F32, name="two_" + who)
-            engine.tensor_tensor(two[:], four[:, 0:2, :], four[:, 2:4, :], ALU.add)
-            one = work.tile([C, CHUNK], F32, name="one_" + who)
-            engine.tensor_tensor(one[:], two[:, 0, :], two[:, 1, :], ALU.add)
-            return one
-
-        for i in range(NCHUNK):
+        def weighted_sum(i):
             j0 = i * CHUNK
             weighted = work.tile([C, U, G, CHUNK], F32, name="weighted")
+            late = psum_held.tile([C, CHUNK], F32, name="late")
             for u in range(U):
                 attn_c = psum_ring.tile([C, G, CHUNK], F32, name="attn_c")
-                for g in range(G):
-                    nc.tensor.matmul(
-                        attn_c[:, g, :], spread[:, u, :, :].rearrange("r h d -> r (h d)"), flipped[i][:, g, :]
-                    )
+                nc.tensor.matmul(
+                    attn_c[:].rearrange("c g j -> c (g j)"),
+                    spread[:, u, :, :].rearrange("r h d -> r (h d)"),
+                    flipped[i][:].rearrange("r g j -> r (g j)"),
+                )
                 nc.vector.tensor_tensor(
                     weighted[:, u], attn_c[:], nbr[i][:].rearrange("c (g u) j -> c u g j", g=G)[:, u], ALU.mult
                 )
-            early = sum_of_eight(nc.gpsimd, weighted[:, 0:4], "pool")
-            early_res = work.tile([C, CHUNK], F32, name="early_res")
-            nc.gpsimd.tensor_tensor(early_res[:], early[:], residual[:, j0 : j0 + CHUNK], ALU.add)
-            late = sum_of_eight(nc.vector, weighted[:, 4:8], "vector")
+            four = work.tile([C, 4, CHUNK], F32, name="four")
+            nc.gpsimd.tensor_tensor(four[:], weighted[:, 0:4, 0, :], weighted[:, 0:4, 1, :], ALU.add)
+            two = work.tile([C, 2, CHUNK], F32, name="two")
+            nc.gpsimd.tensor_tensor(two[:], four[:, 0:2, :], four[:, 2:4, :], ALU.add)
+            one = work.tile([C, CHUNK], F32, name="one")
+            nc.gpsimd.tensor_tensor(one[:], two[:, 0, :], two[:, 1, :], ALU.add)
+            early = work.tile([C, CHUNK], F32, name="early")
+            nc.gpsimd.tensor_tensor(early[:], one[:], residual[:, j0 : j0 + CHUNK], ALU.add)
+            for u in range(U // 2, U):
+                for g in range(G):
+                    nc.tensor.matmul(late[:], identity_f[:], weighted[:, u, g, :],
+                                     start=(u == U // 2 and g == 0), stop=(u == U - 1 and g == G - 1))
             result = work.tile([C, CHUNK], F32, name="result")
-            nc.vector.tensor_tensor(result[:], early_res[:], late[:], ALU.add)
+            nc.vector.tensor_tensor(result[:], late[:], early[:], ALU.add)
             nc.sync.dma_start(out[:, j0 : j0 + CHUNK], result[:])
+
+        weights_of(0)
+        for i in range(NCHUNK):
+            if i + 1 < NCHUNK:
+                weights_of(i + 1)
+            weighted_sum(i)

@@ -11,7 +11,6 @@ C, S, N, T, H = 128, 4096, 1024, 16, 4
 DH = C // H
 SCALE = 1.0 / math.sqrt(DH)
 
-BANK = 512
 BLOCK = 128
 CHUNK = 256
 NCHUNK = N // CHUNK
@@ -19,7 +18,10 @@ NBLOCK = CHUNK // BLOCK
 G, U = 2, 8
 PIECES = 3
 ROWS = PIECES * H * U
-T_POOL = 4
+T_POOL = 2
+T_STEP = 2
+BANKS = NCHUNK * U
+AHEAD = 2
 
 FLOPS = 2 * C * C * N + 2 * 2 * C * T * N
 
@@ -30,7 +32,8 @@ def tile_localppftransformer_kernel(tc, f, nb, w_q, b_q, b_o, offs, out):
         tc.tile_pool(name="held", bufs=1) as held,
         tc.tile_pool(name="work", bufs=2) as work,
         tc.psum_pool(name="psum_held", bufs=1) as psum_held,
-        tc.psum_pool(name="psum_ring", bufs=3) as psum_ring,
+        tc.psum_pool(name="psum_query", bufs=2) as psum_query,
+        tc.psum_pool(name="psum_ring", bufs=AHEAD + 1) as psum_ring,
     ):
         offsets = held.tile([C, N // 16], U16, name="offsets")
         nc.sync.dma_start(offsets[:], offs)
@@ -60,59 +63,78 @@ def tile_localppftransformer_kernel(tc, f, nb, w_q, b_q, b_o, offs, out):
         make_identity(nc, identity[:])
         identity_f = held.tile([C, C], F32, name="identity_f")
         make_identity(nc, identity_f[:])
-        spread = held.tile([ROWS, U, H, DH], BF16, name="spread")
-        nc.gpsimd.memset(spread[:], 0.0)
+        pick = held.tile([ROWS, U, H], BF16, name="pick")
+        nc.gpsimd.memset(pick[:], 0.0)
         for piece in range(PIECES):
             nc.gpsimd.affine_select(
-                out=spread[:], in_=spread[:], compare_op=ALU.not_equal, fill=1.0,
-                base=-H * U * piece, channel_multiplier=1, pattern=[[-1, U], [-U, H], [0, DH]],
+                out=pick[:], in_=pick[:], compare_op=ALU.not_equal, fill=1.0,
+                base=-H * U * piece, channel_multiplier=1, pattern=[[-1, U], [-U, H]],
             )
+        spread = held.tile([ROWS, U, H, DH], BF16, name="spread")
+        nc.scalar.copy(spread[:], pick[:].unsqueeze(3).to_broadcast([ROWS, U, H, DH]))
 
         fn = held.tile([C, N], F32, name="fn")
         fn_bf = held.tile([C, N], BF16, name="fn_bf")
         q_sbuf = held.tile([C, N], F32, name="q_sbuf")
         residual = held.tile([C, N], F32, name="residual")
-        q_psum = []
-        for k in range(N // BANK):
-            piece_of_list = offsets[:, k * (BANK // 16) : (k + 1) * (BANK // 16)]
-            columns = slice(k * BANK, (k + 1) * BANK)
+        of = {}
+
+        def live(i):
+            return 0 <= i < NCHUNK
+
+        def look_up(i):
+            if not live(i):
+                return
+            columns = slice(i * CHUNK, (i + 1) * CHUNK)
+            piece_of_list = offsets[:, i * CHUNK // 16 : (i + 1) * CHUNK // 16]
             nc.scalar.activation(fn[:, columns], table[:].indirect(piece_of_list), ACT.Copy)
             nc.scalar.copy(fn_bf[:, columns], fn[:, columns])
-            q_bank = psum_held.tile([C, BANK], F32, name=f"q_bank{k}")
-            nc.tensor.matmul(q_bank[:], wq[:], fn_bf[:, columns])
-            q_psum.append(q_bank)
-            nc.scalar.activation(q_sbuf[:, columns], q_bank[:], ACT.Identity, bias=bq[:, 0:1])
-        nc.scalar.activation(residual[:], fn[:], ACT.Identity, bias=bo[:, 0:1])
+            q_psum = psum_query.tile([C, CHUNK], F32, name="q_psum")
+            nc.tensor.matmul(q_psum[:], wq[:], fn_bf[:, columns])
+            of["q_psum", i] = q_psum
+            nc.scalar.activation(q_sbuf[:, columns], q_psum[:], ACT.Identity, bias=bq[:, 0:1])
+            nc.scalar.activation(residual[:, columns], fn[:, columns], ACT.Identity, bias=bo[:, 0:1])
 
-        flipped = []
-
-        def weights_of(i):
-            j0 = i * CHUNK
-
-            prod = work.tile([C, T, CHUNK], BF16, name="prod")
+        def products_pool(i, g):
+            if not live(i):
+                return
+            if g == 0:
+                of["prod", i] = work.tile([C, T, CHUNK], BF16, name="prod")
+            lo = g * U
             nc.gpsimd.tensor_tensor(
-                prod[:, 0:T_POOL, :],
-                q_sbuf[:, j0 : j0 + CHUNK].unsqueeze(1).to_broadcast([C, T_POOL, CHUNK]),
-                nbr[i][:, 0:T_POOL, :],
+                of["prod", i][:, lo : lo + T_POOL, :],
+                q_sbuf[:, i * CHUNK : (i + 1) * CHUNK].unsqueeze(1).to_broadcast([C, T_POOL, CHUNK]),
+                nbr[i][:, lo : lo + T_POOL, :],
                 ALU.mult,
             )
-            for lo, hi in ((T_POOL, U), (U, T)):
-                nc.vector.scalar_tensor_tensor(
-                    out=prod[:, lo:hi, :],
-                    in0=q_psum[j0 // BANK][:, j0 % BANK : j0 % BANK + CHUNK].unsqueeze(1).to_broadcast([C, hi - lo, CHUNK]),
-                    scalar=bq[:, 0:1],
-                    in1=nbr[i][:, lo:hi, :],
-                    op0=ALU.add, op1=ALU.mult,
-                )
 
-            score = psum_held.tile([BLOCK, NBLOCK, G, H, U], F32, name="score")
-            for g in range(G):
-                for u in range(U):
-                    for b in range(NBLOCK):
-                        nc.tensor.matmul(
-                            score[:, b, g, :, u], prod[:, g * U + u, b * BLOCK : (b + 1) * BLOCK], head_of[:]
-                        )
+        def products_vector(i, g, step):
+            if not live(i):
+                return
+            lo = g * U + T_POOL + step * T_STEP
+            nc.vector.scalar_tensor_tensor(
+                out=of["prod", i][:, lo : lo + T_STEP, :],
+                in0=of["q_psum", i][:].unsqueeze(1).to_broadcast([C, T_STEP, CHUNK]),
+                scalar=bq[:, 0:1],
+                in1=nbr[i][:, lo : lo + T_STEP, :],
+                op0=ALU.add, op1=ALU.mult,
+            )
 
+        def scores(i, g):
+            if not live(i):
+                return
+            if g == 0:
+                of["score", i] = psum_held.tile([BLOCK, NBLOCK, G, H, U], F32, name="score")
+            for u in range(U):
+                for b in range(NBLOCK):
+                    nc.tensor.matmul(
+                        of["score", i][:, b, g, :, u], of["prod", i][:, g * U + u, b * BLOCK : (b + 1) * BLOCK], head_of[:]
+                    )
+
+        def exponentials(i):
+            if not live(i):
+                return
+            score = of["score", i]
             neg_max = work.tile([BLOCK, NBLOCK, H], F32, name="neg_max")
             nc.vector.tensor_reduce(
                 out=neg_max[:], in_=score[:].rearrange("p b g h u -> p b h g u"),
@@ -120,74 +142,130 @@ def tile_localppftransformer_kernel(tc, f, nb, w_q, b_q, b_o, offs, out):
             )
             shift = work.tile([BLOCK, NBLOCK, H], F32, name="shift")
             nc.scalar.mul(shift[:], neg_max[:], SCALE)
-            expo = work.tile([BLOCK, NBLOCK, G, H, U], F32, name="expo")
-            total = work.tile([BLOCK, NBLOCK, H], F32, name="total")
+            of["expo", i] = work.tile([BLOCK, NBLOCK, G, H, U], F32, name="expo")
+            of["total", i] = work.tile([BLOCK, NBLOCK, H], F32, name="total")
             for b in range(NBLOCK):
                 for h in range(H):
                     nc.scalar.activation(
-                        expo[:, b, :, h, :], score[:, b, :, h, :], ACT.Exp,
-                        bias=shift[:, b, h : h + 1], scale=SCALE, accum_out=total[:, b, h : h + 1],
+                        of["expo", i][:, b, :, h, :], score[:, b, :, h, :], ACT.Exp,
+                        bias=shift[:, b, h : h + 1], scale=SCALE, accum_out=of["total", i][:, b, h : h + 1],
                     )
+
+        def normalised(i):
+            if not live(i):
+                return
             inverse = work.tile([BLOCK, NBLOCK, H], F32, name="inverse")
-            nc.vector.reciprocal(inverse[:], total[:])
+            nc.vector.reciprocal(inverse[:], of["total", i][:])
             attn = work.tile([BLOCK, NBLOCK, G, H, U], F32, name="attn")
             for b in range(NBLOCK):
                 for h in range(H):
                     nc.scalar.activation(
-                        attn[:, b, :, h, :], expo[:, b, :, h, :], ACT.Copy, scale=inverse[:, b, h : h + 1]
+                        attn[:, b, :, h, :], of["expo", i][:, b, :, h, :], ACT.Copy, scale=inverse[:, b, h : h + 1]
                     )
+            of["attn", i] = attn[:].rearrange("p b g h u -> p (b g) (h u)")
+            of["pieces", i] = work.tile([BLOCK, NBLOCK * G, PIECES, H * U], BF16, name="pieces")
+            nc.scalar.copy(of["pieces", i][:, :, 0, :], of["attn", i])
 
-            attn_flat = attn[:].rearrange("p b g h u -> p (b g) (h u)")
-            pieces = work.tile([BLOCK, NBLOCK * G, PIECES, H * U], BF16, name="pieces")
-            rest = work.tile([BLOCK, NBLOCK * G, H * U], F32, name="rest")
-            nc.scalar.copy(pieces[:, :, 0, :], attn_flat)
-            nc.gpsimd.tensor_tensor(rest[:], attn_flat, pieces[:, :, 0, :], ALU.subtract)
-            nc.gpsimd.tensor_copy(pieces[:, :, 1, :], rest[:])
-            nc.gpsimd.tensor_tensor(pieces[:, :, 2, :], rest[:], pieces[:, :, 1, :], ALU.subtract)
+        def second_piece(i):
+            if not live(i):
+                return
+            of["rest", i] = work.tile([BLOCK, NBLOCK * G, H * U], F32, name="rest")
+            nc.gpsimd.tensor_tensor(of["rest", i][:], of["attn", i], of["pieces", i][:, :, 0, :], ALU.subtract)
+            nc.scalar.copy(of["pieces", i][:, :, 1, :], of["rest", i][:])
 
+        def third_piece(i):
+            if not live(i):
+                return
+            nc.gpsimd.tensor_tensor(
+                of["pieces", i][:, :, 2, :], of["rest", i][:], of["pieces", i][:, :, 1, :], ALU.subtract
+            )
+
+        def flipped(i):
+            if not live(i):
+                return
             flipped_ps = psum_held.tile([ROWS, G, CHUNK], BF16, name="flipped_ps")
             for b in range(NBLOCK):
                 for g in range(G):
                     nc.tensor.transpose(
                         flipped_ps[:, g, b * BLOCK : (b + 1) * BLOCK],
-                        pieces[:, b * G + g, :, :].rearrange("p k x -> p (k x)"),
+                        of["pieces", i][:, b * G + g, :, :].rearrange("p k x -> p (k x)"),
                         identity[:],
                     )
-            flipped.append(held.tile([ROWS, G, CHUNK], BF16, name=f"flipped{i}"))
-            nc.scalar.copy(flipped[i][:], flipped_ps[:])
+            of["flipped", i] = work.tile([ROWS, G, CHUNK], BF16, name="flipped")
+            nc.scalar.copy(of["flipped", i][:], flipped_ps[:])
 
-        def weighted_sum(i):
-            j0 = i * CHUNK
-            weighted = work.tile([C, U, G, CHUNK], F32, name="weighted")
-            late = psum_held.tile([C, CHUNK], F32, name="late")
-            for u in range(U):
-                attn_c = psum_ring.tile([C, G, CHUNK], F32, name="attn_c")
-                nc.tensor.matmul(
-                    attn_c[:].rearrange("c g j -> c (g j)"),
-                    spread[:, u, :, :].rearrange("r h d -> r (h d)"),
-                    flipped[i][:].rearrange("r g j -> r (g j)"),
-                )
-                nc.vector.tensor_tensor(
-                    weighted[:, u], attn_c[:], nbr[i][:].rearrange("c (g u) j -> c u g j", g=G)[:, u], ALU.mult
-                )
-            four = work.tile([C, 4, CHUNK], F32, name="four")
-            nc.gpsimd.tensor_tensor(four[:], weighted[:, 0:4, 0, :], weighted[:, 0:4, 1, :], ALU.add)
-            two = work.tile([C, 2, CHUNK], F32, name="two")
-            nc.gpsimd.tensor_tensor(two[:], four[:, 0:2, :], four[:, 2:4, :], ALU.add)
-            one = work.tile([C, CHUNK], F32, name="one")
-            nc.gpsimd.tensor_tensor(one[:], two[:, 0, :], two[:, 1, :], ALU.add)
-            early = work.tile([C, CHUNK], F32, name="early")
-            nc.gpsimd.tensor_tensor(early[:], one[:], residual[:, j0 : j0 + CHUNK], ALU.add)
-            for u in range(U // 2, U):
-                for g in range(G):
-                    nc.tensor.matmul(late[:], identity_f[:], weighted[:, u, g, :],
-                                     start=(u == U // 2 and g == 0), stop=(u == U - 1 and g == G - 1))
+        def spread_out(n):
+            if not 0 <= n < BANKS:
+                return
+            i, u = divmod(n, U)
+            of["attn_c", n] = psum_ring.tile([C, G, CHUNK], F32, name="attn_c")
+            nc.tensor.matmul(
+                of["attn_c", n][:].rearrange("c g j -> c (g j)"),
+                spread[:, u, :, :].rearrange("r h d -> r (h d)"),
+                of["flipped", i][:].rearrange("r g j -> r (g j)"),
+            )
+
+        def multiplied(n):
+            if not 0 <= n < BANKS:
+                return
+            i, u = divmod(n, U)
+            if u == 0:
+                of["terms", i] = work.tile([C, U, G, CHUNK], F32, name="terms")
+            nc.vector.tensor_tensor(
+                of["terms", i][:, u], of["attn_c", n][:], nbr[i][:].rearrange("c (g u) j -> c u g j", g=G)[:, u], ALU.mult
+            )
+
+        def added(n):
+            if not 0 <= n < BANKS:
+                return
+            i, u = divmod(n, U)
+            if u == 0:
+                of["early", i] = work.tile([C, CHUNK], F32, name="early")
+                of["late", i] = psum_held.tile([C, CHUNK], F32, name="late")
+            so_far = residual[:, i * CHUNK : (i + 1) * CHUNK] if u == 0 else of["early", i][:]
+            nc.gpsimd.tensor_tensor(of["early", i][:], so_far, of["terms", i][:, u, 0, :], ALU.add)
+            nc.tensor.matmul(of["late", i][:], identity_f[:], of["terms", i][:, u, 1, :], start=(u == 0), stop=(u == U - 1))
+
+        def finished(i):
+            if not live(i):
+                return
             result = work.tile([C, CHUNK], F32, name="result")
-            nc.vector.tensor_tensor(result[:], late[:], early[:], ALU.add)
-            nc.sync.dma_start(out[:, j0 : j0 + CHUNK], result[:])
+            nc.vector.tensor_tensor(result[:], of["late", i][:], of["early", i][:], ALU.add)
+            nc.sync.dma_start(out[:, i * CHUNK : (i + 1) * CHUNK], result[:])
 
-        weights_of(0)
-        for i in range(NCHUNK):
-            if i + 1 < NCHUNK:
-                weights_of(i + 1)
-            weighted_sum(i)
+        look_up(0)
+        look_up(1)
+        for p in range(NCHUNK + 3):
+            first = U * (p - 2)
+
+            def tick(k):
+                multiplied(first + k)
+                spread_out(first + k + AHEAD)
+                if k == 1:
+                    finished(p - 3)
+                added(first + k - 1)
+
+            tick(0)
+            exponentials(p - 1)
+            products_pool(p, 0)
+            products_vector(p, 0, 0)
+            tick(1)
+            normalised(p - 1)
+            products_vector(p, 0, 1)
+            tick(2)
+            second_piece(p - 1)
+            products_vector(p, 0, 2)
+            tick(3)
+            third_piece(p - 1)
+            scores(p, 0)
+            products_pool(p, 1)
+            products_vector(p, 1, 0)
+            tick(4)
+            flipped(p - 1)
+            products_vector(p, 1, 1)
+            tick(5)
+            products_vector(p, 1, 2)
+            tick(6)
+            scores(p, 1)
+            tick(7)
+            look_up(p + 2)

@@ -32,7 +32,7 @@ def tile_localppftransformer_kernel(tc, f, nb, w_q, b_q, b_o, offs, out):
         tc.tile_pool(name="held", bufs=1) as held,
         tc.tile_pool(name="work", bufs=2) as work,
         tc.psum_pool(name="psum_held", bufs=1) as psum_held,
-        tc.psum_pool(name="psum_query", bufs=2) as psum_query,
+        tc.psum_pool(name="psum_wide", bufs=3) as psum_wide,
         tc.psum_pool(name="psum_ring", bufs=AHEAD + 1) as psum_ring,
     ):
         offsets = held.tile([C, N // 16], U16, name="offsets")
@@ -76,7 +76,6 @@ def tile_localppftransformer_kernel(tc, f, nb, w_q, b_q, b_o, offs, out):
         fn = held.tile([C, N], F32, name="fn")
         fn_bf = held.tile([C, N], BF16, name="fn_bf")
         q_sbuf = held.tile([C, N], F32, name="q_sbuf")
-        residual = held.tile([C, N], F32, name="residual")
         of = {}
 
         def live(i):
@@ -89,11 +88,10 @@ def tile_localppftransformer_kernel(tc, f, nb, w_q, b_q, b_o, offs, out):
             piece_of_list = offsets[:, i * CHUNK // 16 : (i + 1) * CHUNK // 16]
             nc.scalar.activation(fn[:, columns], table[:].indirect(piece_of_list), ACT.Copy)
             nc.scalar.copy(fn_bf[:, columns], fn[:, columns])
-            q_psum = psum_query.tile([C, CHUNK], F32, name="q_psum")
+            q_psum = psum_wide.tile([C, CHUNK], F32, name="q_psum", tag="wide")
             nc.tensor.matmul(q_psum[:], wq[:], fn_bf[:, columns])
             of["q_psum", i] = q_psum
             nc.scalar.activation(q_sbuf[:, columns], q_psum[:], ACT.Identity, bias=bq[:, 0:1])
-            nc.scalar.activation(residual[:, columns], fn[:, columns], ACT.Identity, bias=bo[:, 0:1])
 
         def products_pool(i, g):
             if not live(i):
@@ -215,22 +213,39 @@ def tile_localppftransformer_kernel(tc, f, nb, w_q, b_q, b_o, offs, out):
                 of["terms", i][:, u], of["attn_c", n][:], nbr[i][:].rearrange("c (g u) j -> c u g j", g=G)[:, u], ALU.mult
             )
 
+        def transposed_onto(total, i, block, what, first=False, last=False):
+            nc.tensor.matmul(total[:, block, :], what, identity_f[:], start=first, stop=last, is_transpose=True)
+
         def added(n):
             if not 0 <= n < BANKS:
                 return
             i, u = divmod(n, U)
             if u == 0:
-                of["early", i] = work.tile([C, CHUNK], F32, name="early")
-                of["late", i] = psum_held.tile([C, CHUNK], F32, name="late")
-            so_far = residual[:, i * CHUNK : (i + 1) * CHUNK] if u == 0 else of["early", i][:]
-            nc.gpsimd.tensor_tensor(of["early", i][:], so_far, of["terms", i][:, u, 0, :], ALU.add)
-            nc.tensor.matmul(of["late", i][:], identity_f[:], of["terms", i][:, u, 1, :], start=(u == 0), stop=(u == U - 1))
+                of["sum", i] = psum_wide.tile([BLOCK, NBLOCK, C], F32, name="sum_t", tag="wide")
+                for b in range(NBLOCK):
+                    j0 = i * CHUNK + b * BLOCK
+                    transposed_onto(of["sum", i], i, b, fn[:, j0 : j0 + BLOCK], first=(b == 0))
+            for g in range(G):
+                for b in range(NBLOCK):
+                    transposed_onto(
+                        of["sum", i], i, b, of["terms", i][:, u, g, b * BLOCK : (b + 1) * BLOCK],
+                        last=(u == U - 1 and g == G - 1 and b == NBLOCK - 1),
+                    )
+
+        def copied_out(i):
+            if not live(i):
+                return
+            of["sum_sbuf", i] = work.tile([BLOCK, NBLOCK, C], F32, name="sum_sbuf")
+            nc.scalar.copy(of["sum_sbuf", i][:], of["sum", i][:])
 
         def finished(i):
             if not live(i):
                 return
+            back = psum_wide.tile([C, CHUNK], F32, name="back", tag="wide")
+            for b in range(NBLOCK):
+                nc.tensor.transpose(back[:, b * BLOCK : (b + 1) * BLOCK], of["sum_sbuf", i][:, b, :], identity_f[:])
             result = work.tile([C, CHUNK], F32, name="result")
-            nc.vector.tensor_tensor(result[:], of["late", i][:], of["early", i][:], ALU.add)
+            nc.scalar.activation(result[:], back[:], ACT.Identity, bias=bo[:, 0:1])
             nc.sync.dma_start(out[:, i * CHUNK : (i + 1) * CHUNK], result[:])
 
         look_up(0)
@@ -241,11 +256,10 @@ def tile_localppftransformer_kernel(tc, f, nb, w_q, b_q, b_o, offs, out):
             def tick(k):
                 multiplied(first + k)
                 spread_out(first + k + AHEAD)
-                if k == 1:
-                    finished(p - 3)
                 added(first + k - 1)
 
             tick(0)
+            copied_out(p - 3)
             exponentials(p - 1)
             products_pool(p, 0)
             products_vector(p, 0, 0)
@@ -253,6 +267,7 @@ def tile_localppftransformer_kernel(tc, f, nb, w_q, b_q, b_o, offs, out):
             normalised(p - 1)
             products_vector(p, 0, 1)
             tick(2)
+            finished(p - 3)
             second_piece(p - 1)
             products_vector(p, 0, 2)
             tick(3)

@@ -18,10 +18,11 @@ NBLOCK = CHUNK // BLOCK
 G, U = 2, 8
 PIECES = 3
 ROWS = PIECES * H * U
-T_POOL = 2
-T_STEP = 2
+T_POOL = 3
 BANKS = NCHUNK * U
 AHEAD = 2
+LAG = 6
+TICKS = U // G
 
 FLOPS = 2 * C * C * N + 2 * 2 * C * T * N
 
@@ -81,17 +82,21 @@ def tile_localppftransformer_kernel(tc, f, nb, w_q, b_q, b_o, offs, out):
         def live(i):
             return 0 <= i < NCHUNK
 
-        def look_up(i):
-            if not live(i):
-                return
+        def looked_up(i):
             columns = slice(i * CHUNK, (i + 1) * CHUNK)
             piece_of_list = offsets[:, i * CHUNK // 16 : (i + 1) * CHUNK // 16]
             nc.scalar.activation(fn[:, columns], table[:].indirect(piece_of_list), ACT.Copy)
             nc.scalar.copy(fn_bf[:, columns], fn[:, columns])
-            q_psum = psum_wide.tile([C, CHUNK], F32, name="q_psum", tag="wide")
-            nc.tensor.matmul(q_psum[:], wq[:], fn_bf[:, columns])
-            of["q_psum", i] = q_psum
-            nc.scalar.activation(q_sbuf[:, columns], q_psum[:], ACT.Identity, bias=bq[:, 0:1])
+            if i % 2 == 0:
+                of["q_bank", i // 2] = psum_wide.tile([C, 2, CHUNK], F32, name="q_bank", tag="wide")
+            of["q_psum", i] = of["q_bank", i // 2][:, i % 2, :]
+            nc.tensor.matmul(of["q_psum", i], wq[:], fn_bf[:, columns])
+            of["q_again", i] = psum_ring.tile([C, CHUNK], F32, name="q_again", tag="attn_c")
+            nc.tensor.matmul(of["q_again", i][:], wq[:], fn_bf[:, columns])
+
+        def query_copied(i):
+            columns = slice(i * CHUNK, (i + 1) * CHUNK)
+            nc.scalar.activation(q_sbuf[:, columns], of["q_again", i][:], ACT.Identity, bias=bq[:, 0:1])
 
         def products_pool(i, g):
             if not live(i):
@@ -106,15 +111,15 @@ def tile_localppftransformer_kernel(tc, f, nb, w_q, b_q, b_o, offs, out):
                 ALU.mult,
             )
 
-        def products_vector(i, g, step):
+        def products_vector(i, g):
             if not live(i):
                 return
-            lo = g * U + T_POOL + step * T_STEP
+            lo, hi = g * U + T_POOL, (g + 1) * U
             nc.vector.scalar_tensor_tensor(
-                out=of["prod", i][:, lo : lo + T_STEP, :],
-                in0=of["q_psum", i][:].unsqueeze(1).to_broadcast([C, T_STEP, CHUNK]),
+                out=of["prod", i][:, lo:hi, :],
+                in0=of["q_psum", i].unsqueeze(1).to_broadcast([C, hi - lo, CHUNK]),
                 scalar=bq[:, 0:1],
-                in1=nbr[i][:, lo : lo + T_STEP, :],
+                in1=nbr[i][:, lo:hi, :],
                 op0=ALU.add, op1=ALU.mult,
             )
 
@@ -148,21 +153,15 @@ def tile_localppftransformer_kernel(tc, f, nb, w_q, b_q, b_o, offs, out):
                         of["expo", i][:, b, :, h, :], score[:, b, :, h, :], ACT.Exp,
                         bias=shift[:, b, h : h + 1], scale=SCALE, accum_out=of["total", i][:, b, h : h + 1],
                     )
-
-        def normalised(i):
-            if not live(i):
-                return
-            inverse = work.tile([BLOCK, NBLOCK, H], F32, name="inverse")
-            nc.vector.reciprocal(inverse[:], of["total", i][:])
-            attn = work.tile([BLOCK, NBLOCK, G, H, U], F32, name="attn")
-            for b in range(NBLOCK):
-                for h in range(H):
-                    nc.scalar.activation(
-                        attn[:, b, :, h, :], of["expo", i][:, b, :, h, :], ACT.Copy, scale=inverse[:, b, h : h + 1]
-                    )
-            of["attn", i] = attn[:].rearrange("p b g h u -> p (b g) (h u)")
+            of["attn", i] = of["expo", i][:].rearrange("p b g h u -> p (b g) (h u)")
             of["pieces", i] = work.tile([BLOCK, NBLOCK * G, PIECES, H * U], BF16, name="pieces")
             nc.scalar.copy(of["pieces", i][:, :, 0, :], of["attn", i])
+
+        def inverted(i):
+            if not live(i):
+                return
+            of["inverse", i] = held.tile([BLOCK, NBLOCK, H], F32, name=f"inverse{i}")
+            nc.vector.reciprocal(of["inverse", i][:], of["total", i][:])
 
         def second_piece(i):
             if not live(i):
@@ -213,7 +212,7 @@ def tile_localppftransformer_kernel(tc, f, nb, w_q, b_q, b_o, offs, out):
                 of["terms", i][:, u], of["attn_c", n][:], nbr[i][:].rearrange("c (g u) j -> c u g j", g=G)[:, u], ALU.mult
             )
 
-        def transposed_onto(total, i, block, what, first=False, last=False):
+        def transposed_onto(total, block, what, first=False, last=False):
             nc.tensor.matmul(total[:, block, :], what, identity_f[:], start=first, stop=last, is_transpose=True)
 
         def added(n):
@@ -222,65 +221,67 @@ def tile_localppftransformer_kernel(tc, f, nb, w_q, b_q, b_o, offs, out):
             i, u = divmod(n, U)
             if u == 0:
                 of["sum", i] = psum_wide.tile([BLOCK, NBLOCK, C], F32, name="sum_t", tag="wide")
-                for b in range(NBLOCK):
-                    j0 = i * CHUNK + b * BLOCK
-                    transposed_onto(of["sum", i], i, b, fn[:, j0 : j0 + BLOCK], first=(b == 0))
             for g in range(G):
                 for b in range(NBLOCK):
                     transposed_onto(
-                        of["sum", i], i, b, of["terms", i][:, u, g, b * BLOCK : (b + 1) * BLOCK],
-                        last=(u == U - 1 and g == G - 1 and b == NBLOCK - 1),
+                        of["sum", i], b, of["terms", i][:, u, g, b * BLOCK : (b + 1) * BLOCK],
+                        first=(u == 0 and g == 0 and b == 0), last=(u == U - 1 and g == G - 1 and b == NBLOCK - 1),
                     )
 
         def copied_out(i):
             if not live(i):
                 return
             of["sum_sbuf", i] = work.tile([BLOCK, NBLOCK, C], F32, name="sum_sbuf")
-            nc.scalar.copy(of["sum_sbuf", i][:], of["sum", i][:])
+            for b in range(NBLOCK):
+                for h in range(H):
+                    nc.scalar.activation(
+                        of["sum_sbuf", i][:, b, h * DH : (h + 1) * DH], of["sum", i][:, b, h * DH : (h + 1) * DH],
+                        ACT.Copy, scale=of["inverse", i][:, b, h : h + 1],
+                    )
+            of["back", i] = psum_wide.tile([C, CHUNK], F32, name="back", tag="wide")
+            nc.tensor.matmul(of["back", i][:], identity_f[:], fn[:, i * CHUNK : (i + 1) * CHUNK], start=True, stop=False)
 
         def finished(i):
             if not live(i):
                 return
-            back = psum_wide.tile([C, CHUNK], F32, name="back", tag="wide")
             for b in range(NBLOCK):
-                nc.tensor.transpose(back[:, b * BLOCK : (b + 1) * BLOCK], of["sum_sbuf", i][:, b, :], identity_f[:])
+                nc.tensor.matmul(
+                    of["back", i][:, b * BLOCK : (b + 1) * BLOCK], of["sum_sbuf", i][:, b, :], identity_f[:],
+                    start=False, stop=(b == NBLOCK - 1), is_transpose=True,
+                )
             result = work.tile([C, CHUNK], F32, name="result")
-            nc.scalar.activation(result[:], back[:], ACT.Identity, bias=bo[:, 0:1])
+            nc.scalar.activation(result[:], of["back", i][:], ACT.Identity, bias=bo[:, 0:1])
             nc.sync.dma_start(out[:, i * CHUNK : (i + 1) * CHUNK], result[:])
 
-        look_up(0)
-        look_up(1)
-        for p in range(NCHUNK + 3):
-            first = U * (p - 2)
+        looked_up(0)
+        for i in range(1, NCHUNK):
+            looked_up(i)
+            query_copied(i - 1)
+        query_copied(NCHUNK - 1)
 
-            def tick(k):
-                multiplied(first + k)
-                spread_out(first + k + AHEAD)
-                added(first + k - 1)
+        def chunk_of(step):
+            return step // 2 if step % 2 == 0 else -1
 
-            tick(0)
-            copied_out(p - 3)
-            exponentials(p - 1)
-            products_pool(p, 0)
-            products_vector(p, 0, 0)
-            tick(1)
-            normalised(p - 1)
-            products_vector(p, 0, 1)
-            tick(2)
-            finished(p - 3)
-            second_piece(p - 1)
-            products_vector(p, 0, 2)
-            tick(3)
-            third_piece(p - 1)
-            scores(p, 0)
-            products_pool(p, 1)
-            products_vector(p, 1, 0)
-            tick(4)
-            flipped(p - 1)
-            products_vector(p, 1, 1)
-            tick(5)
-            products_vector(p, 1, 2)
-            tick(6)
-            scores(p, 1)
-            tick(7)
-            look_up(p + 2)
+        def tick(n):
+            multiplied(n)
+            spread_out(n + AHEAD)
+            added(n - 1)
+            if n % U == 0:
+                copied_out(n // U - 1)
+            if n % U == 2:
+                finished(n // U - 1)
+
+        for step in range(G * NCHUNK + LAG + 1):
+            n = TICKS * (step - LAG)
+            tick(n)
+            products_pool(step // 2, step % 2)
+            products_vector(step // 2, step % 2)
+            second_piece(chunk_of(step - 3))
+            flipped(chunk_of(step - 4))
+            tick(n + 1)
+            exponentials(chunk_of(step - 2))
+            third_piece(chunk_of(step - 3))
+            inverted(chunk_of(step - 3))
+            tick(n + 2)
+            tick(n + 3)
+            scores(step // 2, step % 2)

@@ -64,15 +64,18 @@ def tile_localppftransformer_kernel(tc, f, nb, w_q, b_q, b_o, offs, out):
         make_identity(nc, identity[:])
         identity_f = held.tile([C, C], F32, name="identity_f")
         make_identity(nc, identity_f[:])
-        pick = held.tile([ROWS, U, H], BF16, name="pick")
+        pick = held.tile([C, U, H], BF16, name="pick")
         nc.gpsimd.memset(pick[:], 0.0)
         for piece in range(PIECES):
             nc.gpsimd.affine_select(
                 out=pick[:], in_=pick[:], compare_op=ALU.not_equal, fill=1.0,
                 base=-H * U * piece, channel_multiplier=1, pattern=[[-1, U], [-U, H]],
             )
-        spread = held.tile([ROWS, U, H, DH], BF16, name="spread")
-        nc.scalar.copy(spread[:], pick[:].unsqueeze(3).to_broadcast([ROWS, U, H, DH]))
+        spread = held.tile([C, U, H, DH], BF16, name="spread")
+        nc.scalar.copy(spread[:], pick[:].unsqueeze(3).to_broadcast([C, U, H, DH]))
+        e_rows = [held.tile([C, G, CHUNK], BF16, name=f"e_rows{i}") for i in range(NCHUNK)]
+        for i in range(NCHUNK):
+            nc.gpsimd.memset(e_rows[i][ROWS:C], 0.0)
 
         fn = held.tile([C, N], F32, name="fn")
         fn_bf = held.tile([C, N], BF16, name="fn_bf")
@@ -188,8 +191,7 @@ def tile_localppftransformer_kernel(tc, f, nb, w_q, b_q, b_o, offs, out):
                         of["pieces", i][:, b * G + g, :, :].rearrange("p k x -> p (k x)"),
                         identity[:],
                     )
-            of["flipped", i] = work.tile([ROWS, G, CHUNK], BF16, name="flipped")
-            nc.scalar.copy(of["flipped", i][:], flipped_ps[:])
+            nc.scalar.copy(e_rows[i][0:ROWS], flipped_ps[:])
 
         def spread_out(n):
             if not 0 <= n < BANKS:
@@ -199,7 +201,7 @@ def tile_localppftransformer_kernel(tc, f, nb, w_q, b_q, b_o, offs, out):
             nc.tensor.matmul(
                 of["attn_c", n][:].rearrange("c g j -> c (g j)"),
                 spread[:, u, :, :].rearrange("r h d -> r (h d)"),
-                of["flipped", i][:].rearrange("r g j -> r (g j)"),
+                e_rows[i][:].rearrange("r g j -> r (g j)"),
             )
 
         def multiplied(n):

@@ -11,18 +11,20 @@ C, S, N, T, H = 128, 4096, 1024, 16, 4
 DH = C // H
 SCALE = 1.0 / math.sqrt(DH)
 
-BLOCK = 128
-CHUNK = 256
+BANK = 512
+CHUNK = 128
 NCHUNK = N // CHUNK
-NBLOCK = CHUNK // BLOCK
+LOOK = 256
 G, U = 2, 8
 PIECES = 3
 ROWS = PIECES * H * U
 T_POOL = 3
-BANKS = NCHUNK * U
+PAIR = BANK // (G * CHUNK)
+BANKS_OF_CHUNK = U // PAIR
+BANKS = NCHUNK * BANKS_OF_CHUNK
 AHEAD = 2
-LAG = 6
-TICKS = U // G
+TICKS = BANKS_OF_CHUNK // G
+LAG = 8
 
 FLOPS = 2 * C * C * N + 2 * 2 * C * T * N
 
@@ -31,7 +33,8 @@ def tile_localppftransformer_kernel(tc, f, nb, w_q, b_q, b_o, offs, out):
     nc = tc.nc
     with (
         tc.tile_pool(name="held", bufs=1) as held,
-        tc.tile_pool(name="work", bufs=2) as work,
+        tc.tile_pool(name="work", bufs=3) as work,
+        tc.tile_pool(name="soft", bufs=4) as soft,
         tc.psum_pool(name="psum_held", bufs=1) as psum_held,
         tc.psum_pool(name="psum_wide", bufs=3) as psum_wide,
         tc.psum_pool(name="psum_ring", bufs=AHEAD + 1) as psum_ring,
@@ -85,21 +88,24 @@ def tile_localppftransformer_kernel(tc, f, nb, w_q, b_q, b_o, offs, out):
         def live(i):
             return 0 <= i < NCHUNK
 
-        def looked_up(i):
-            columns = slice(i * CHUNK, (i + 1) * CHUNK)
-            piece_of_list = offsets[:, i * CHUNK // 16 : (i + 1) * CHUNK // 16]
+        def columns_of(i):
+            return slice(i * CHUNK, (i + 1) * CHUNK)
+
+        def looked_up(k):
+            columns = slice(k * LOOK, (k + 1) * LOOK)
+            piece_of_list = offsets[:, k * LOOK // 16 : (k + 1) * LOOK // 16]
             nc.scalar.activation(fn[:, columns], table[:].indirect(piece_of_list), ACT.Copy)
             nc.scalar.copy(fn_bf[:, columns], fn[:, columns])
-            if i % 2 == 0:
-                of["q_bank", i // 2] = psum_wide.tile([C, 2, CHUNK], F32, name="q_bank", tag="wide")
-            of["q_psum", i] = of["q_bank", i // 2][:, i % 2, :]
-            nc.tensor.matmul(of["q_psum", i], wq[:], fn_bf[:, columns])
-            of["q_again", i] = psum_ring.tile([C, CHUNK], F32, name="q_again", tag="attn_c")
-            nc.tensor.matmul(of["q_again", i][:], wq[:], fn_bf[:, columns])
+            if k % 2 == 0:
+                of["q_bank", k // 2] = psum_wide.tile([C, BANK], F32, name="q_bank", tag="wide")
+            nc.tensor.matmul(of["q_bank", k // 2][:, (k % 2) * LOOK : (k % 2 + 1) * LOOK], wq[:], fn_bf[:, columns])
+            of["q_again", k] = psum_ring.tile([C, LOOK], F32, name="q_again", tag="e_c")
+            nc.tensor.matmul(of["q_again", k][:], wq[:], fn_bf[:, columns])
 
-        def query_copied(i):
-            columns = slice(i * CHUNK, (i + 1) * CHUNK)
-            nc.scalar.activation(q_sbuf[:, columns], of["q_again", i][:], ACT.Identity, bias=bq[:, 0:1])
+        def query_copied(k):
+            nc.scalar.activation(
+                q_sbuf[:, k * LOOK : (k + 1) * LOOK], of["q_again", k][:], ACT.Identity, bias=bq[:, 0:1]
+            )
 
         def products_pool(i, g):
             if not live(i):
@@ -109,7 +115,7 @@ def tile_localppftransformer_kernel(tc, f, nb, w_q, b_q, b_o, offs, out):
             lo = g * U
             nc.gpsimd.tensor_tensor(
                 of["prod", i][:, lo : lo + T_POOL, :],
-                q_sbuf[:, i * CHUNK : (i + 1) * CHUNK].unsqueeze(1).to_broadcast([C, T_POOL, CHUNK]),
+                q_sbuf[:, columns_of(i)].unsqueeze(1).to_broadcast([C, T_POOL, CHUNK]),
                 nbr[i][:, lo : lo + T_POOL, :],
                 ALU.mult,
             )
@@ -118,9 +124,10 @@ def tile_localppftransformer_kernel(tc, f, nb, w_q, b_q, b_o, offs, out):
             if not live(i):
                 return
             lo, hi = g * U + T_POOL, (g + 1) * U
+            at = i * CHUNK % BANK
             nc.vector.scalar_tensor_tensor(
                 out=of["prod", i][:, lo:hi, :],
-                in0=of["q_psum", i].unsqueeze(1).to_broadcast([C, hi - lo, CHUNK]),
+                in0=of["q_bank", i * CHUNK // BANK][:, at : at + CHUNK].unsqueeze(1).to_broadcast([C, hi - lo, CHUNK]),
                 scalar=bq[:, 0:1],
                 in1=nbr[i][:, lo:hi, :],
                 op0=ALU.add, op1=ALU.mult,
@@ -130,47 +137,43 @@ def tile_localppftransformer_kernel(tc, f, nb, w_q, b_q, b_o, offs, out):
             if not live(i):
                 return
             if g == 0:
-                of["score", i] = psum_held.tile([BLOCK, NBLOCK, G, H, U], F32, name="score")
+                of["score", i] = psum_held.tile([CHUNK, G, H, U], F32, name="score")
             for u in range(U):
-                for b in range(NBLOCK):
-                    nc.tensor.matmul(
-                        of["score", i][:, b, g, :, u], of["prod", i][:, g * U + u, b * BLOCK : (b + 1) * BLOCK], head_of[:]
-                    )
+                nc.tensor.matmul(of["score", i][:, g, :, u], of["prod", i][:, g * U + u, :], head_of[:])
 
         def exponentials(i):
             if not live(i):
                 return
             score = of["score", i]
-            neg_max = work.tile([BLOCK, NBLOCK, H], F32, name="neg_max")
+            neg_max = soft.tile([CHUNK, H], F32, name="neg_max")
             nc.vector.tensor_reduce(
-                out=neg_max[:], in_=score[:].rearrange("p b g h u -> p b h g u"),
+                out=neg_max[:], in_=score[:].rearrange("p g h u -> p h g u"),
                 axis=mybir.AxisListType.XY, op=ALU.max, negate=True,
             )
-            shift = work.tile([BLOCK, NBLOCK, H], F32, name="shift")
+            shift = soft.tile([CHUNK, H], F32, name="shift")
             nc.scalar.mul(shift[:], neg_max[:], SCALE)
-            of["expo", i] = work.tile([BLOCK, NBLOCK, G, H, U], F32, name="expo")
-            of["total", i] = work.tile([BLOCK, NBLOCK, H], F32, name="total")
-            for b in range(NBLOCK):
-                for h in range(H):
-                    nc.scalar.activation(
-                        of["expo", i][:, b, :, h, :], score[:, b, :, h, :], ACT.Exp,
-                        bias=shift[:, b, h : h + 1], scale=SCALE, accum_out=of["total", i][:, b, h : h + 1],
-                    )
-            of["attn", i] = of["expo", i][:].rearrange("p b g h u -> p (b g) (h u)")
-            of["pieces", i] = work.tile([BLOCK, NBLOCK * G, PIECES, H * U], BF16, name="pieces")
-            nc.scalar.copy(of["pieces", i][:, :, 0, :], of["attn", i])
+            e = soft.tile([CHUNK, G, H, U], F32, name="e")
+            of["total", i] = soft.tile([CHUNK, H], F32, name="total")
+            for h in range(H):
+                nc.scalar.activation(
+                    e[:, :, h, :], score[:, :, h, :], ACT.Exp,
+                    bias=shift[:, h : h + 1], scale=SCALE, accum_out=of["total", i][:, h : h + 1],
+                )
+            of["e", i] = e[:].rearrange("p g h u -> p g (h u)")
+            of["pieces", i] = soft.tile([CHUNK, G, PIECES, H * U], BF16, name="pieces")
+            nc.scalar.copy(of["pieces", i][:, :, 0, :], of["e", i])
 
         def inverted(i):
             if not live(i):
                 return
-            of["inverse", i] = held.tile([BLOCK, NBLOCK, H], F32, name=f"inverse{i}")
+            of["inverse", i] = held.tile([CHUNK, H], F32, name=f"inverse{i}")
             nc.vector.reciprocal(of["inverse", i][:], of["total", i][:])
 
         def second_piece(i):
             if not live(i):
                 return
-            of["rest", i] = work.tile([BLOCK, NBLOCK * G, H * U], F32, name="rest")
-            nc.gpsimd.tensor_tensor(of["rest", i][:], of["attn", i], of["pieces", i][:, :, 0, :], ALU.subtract)
+            of["rest", i] = soft.tile([CHUNK, G, H * U], F32, name="rest")
+            nc.gpsimd.tensor_tensor(of["rest", i][:], of["e", i], of["pieces", i][:, :, 0, :], ALU.subtract)
             nc.scalar.copy(of["pieces", i][:, :, 1, :], of["rest", i][:])
 
         def third_piece(i):
@@ -184,82 +187,74 @@ def tile_localppftransformer_kernel(tc, f, nb, w_q, b_q, b_o, offs, out):
             if not live(i):
                 return
             flipped_ps = psum_held.tile([ROWS, G, CHUNK], BF16, name="flipped_ps")
-            for b in range(NBLOCK):
-                for g in range(G):
-                    nc.tensor.transpose(
-                        flipped_ps[:, g, b * BLOCK : (b + 1) * BLOCK],
-                        of["pieces", i][:, b * G + g, :, :].rearrange("p k x -> p (k x)"),
-                        identity[:],
-                    )
+            for g in range(G):
+                nc.tensor.transpose(
+                    flipped_ps[:, g, :], of["pieces", i][:, g, :, :].rearrange("p k x -> p (k x)"), identity[:]
+                )
             nc.scalar.copy(e_rows[i][0:ROWS], flipped_ps[:])
 
         def spread_out(n):
             if not 0 <= n < BANKS:
                 return
-            i, u = divmod(n, U)
-            of["attn_c", n] = psum_ring.tile([C, G, CHUNK], F32, name="attn_c")
-            nc.tensor.matmul(
-                of["attn_c", n][:].rearrange("c g j -> c (g j)"),
-                spread[:, u, :, :].rearrange("r h d -> r (h d)"),
-                e_rows[i][:].rearrange("r g j -> r (g j)"),
-            )
+            i, k = divmod(n, BANKS_OF_CHUNK)
+            of["e_c", n] = psum_ring.tile([C, PAIR, G, CHUNK], F32, name="e_c")
+            for v in range(PAIR):
+                nc.tensor.matmul(
+                    of["e_c", n][:, v].rearrange("c g j -> c (g j)"),
+                    spread[:, PAIR * k + v, :, :].rearrange("r h d -> r (h d)"),
+                    e_rows[i][:].rearrange("r g j -> r (g j)"),
+                )
 
         def multiplied(n):
             if not 0 <= n < BANKS:
                 return
-            i, u = divmod(n, U)
-            if u == 0:
+            i, k = divmod(n, BANKS_OF_CHUNK)
+            if k == 0:
                 of["terms", i] = work.tile([C, U, G, CHUNK], F32, name="terms")
+            us = slice(PAIR * k, PAIR * (k + 1))
             nc.vector.tensor_tensor(
-                of["terms", i][:, u], of["attn_c", n][:], nbr[i][:].rearrange("c (g u) j -> c u g j", g=G)[:, u], ALU.mult
+                of["terms", i][:, us], of["e_c", n][:], nbr[i][:].rearrange("c (g u) j -> c u g j", g=G)[:, us], ALU.mult
             )
-
-        def transposed_onto(total, block, what, first=False, last=False):
-            nc.tensor.matmul(total[:, block, :], what, identity_f[:], start=first, stop=last, is_transpose=True)
 
         def added(n):
             if not 0 <= n < BANKS:
                 return
-            i, u = divmod(n, U)
-            if u == 0:
-                of["sum", i] = psum_wide.tile([BLOCK, NBLOCK, C], F32, name="sum_t", tag="wide")
-            for g in range(G):
-                for b in range(NBLOCK):
-                    transposed_onto(
-                        of["sum", i], b, of["terms", i][:, u, g, b * BLOCK : (b + 1) * BLOCK],
-                        first=(u == 0 and g == 0 and b == 0), last=(u == U - 1 and g == G - 1 and b == NBLOCK - 1),
+            i, k = divmod(n, BANKS_OF_CHUNK)
+            if k == 0:
+                of["sums", i] = psum_wide.tile([C, 2, CHUNK], F32, name="sums", tag="wide")
+            for u in range(PAIR * k, PAIR * (k + 1)):
+                for g in range(G):
+                    nc.tensor.matmul(
+                        of["sums", i][:, 0, :], of["terms", i][:, u, g, :], identity_f[:],
+                        start=(u == 0 and g == 0), stop=(u == U - 1 and g == G - 1), is_transpose=True,
                     )
 
         def copied_out(i):
             if not live(i):
                 return
-            of["sum_sbuf", i] = work.tile([BLOCK, NBLOCK, C], F32, name="sum_sbuf")
-            for b in range(NBLOCK):
-                for h in range(H):
-                    nc.scalar.activation(
-                        of["sum_sbuf", i][:, b, h * DH : (h + 1) * DH], of["sum", i][:, b, h * DH : (h + 1) * DH],
-                        ACT.Copy, scale=of["inverse", i][:, b, h : h + 1],
-                    )
-            of["back", i] = psum_wide.tile([C, CHUNK], F32, name="back", tag="wide")
-            nc.tensor.matmul(of["back", i][:], identity_f[:], fn[:, i * CHUNK : (i + 1) * CHUNK], start=True, stop=False)
+            of["sum_sbuf", i] = work.tile([CHUNK, C], F32, name="sum_sbuf")
+            for h in range(H):
+                nc.scalar.activation(
+                    of["sum_sbuf", i][:, h * DH : (h + 1) * DH], of["sums", i][:, 0, h * DH : (h + 1) * DH],
+                    ACT.Copy, scale=of["inverse", i][:, h : h + 1],
+                )
 
         def finished(i):
             if not live(i):
                 return
-            for b in range(NBLOCK):
-                nc.tensor.matmul(
-                    of["back", i][:, b * BLOCK : (b + 1) * BLOCK], of["sum_sbuf", i][:, b, :], identity_f[:],
-                    start=False, stop=(b == NBLOCK - 1), is_transpose=True,
-                )
+            nc.tensor.matmul(of["sums", i][:, 1, :], identity_f[:], fn[:, columns_of(i)], start=True, stop=False)
+            nc.tensor.matmul(
+                of["sums", i][:, 1, :], of["sum_sbuf", i][:], identity_f[:], start=False, stop=True, is_transpose=True
+            )
             result = work.tile([C, CHUNK], F32, name="result")
-            nc.scalar.activation(result[:], of["back", i][:], ACT.Identity, bias=bo[:, 0:1])
-            nc.sync.dma_start(out[:, i * CHUNK : (i + 1) * CHUNK], result[:])
+            nc.scalar.activation(result[:], of["sums", i][:, 1, :], ACT.Identity, bias=bo[:, 0:1])
+            nc.sync.dma_start(out[:, columns_of(i)], result[:])
 
         looked_up(0)
-        for i in range(1, NCHUNK):
-            looked_up(i)
-            query_copied(i - 1)
-        query_copied(NCHUNK - 1)
+        for k in range(1, N // LOOK):
+            looked_up(k)
+            query_copied(k - 1)
+        query_copied(N // LOOK - 1)
 
         def chunk_of(step):
             return step // 2 if step % 2 == 0 else -1
@@ -268,22 +263,20 @@ def tile_localppftransformer_kernel(tc, f, nb, w_q, b_q, b_o, offs, out):
             multiplied(n)
             spread_out(n + AHEAD)
             added(n - 1)
-            if n % U == 0:
-                copied_out(n // U - 1)
-            if n % U == 2:
-                finished(n // U - 1)
+            if n % BANKS_OF_CHUNK == 0:
+                copied_out(n // BANKS_OF_CHUNK - 1)
+            if n % BANKS_OF_CHUNK == 2:
+                finished(n // BANKS_OF_CHUNK - 1)
 
-        for step in range(G * NCHUNK + LAG + 1):
+        for step in range(G * NCHUNK + LAG + 2):
             n = TICKS * (step - LAG)
             tick(n)
+            exponentials(chunk_of(step - 2))
+            second_piece(chunk_of(step - 3))
+            third_piece(chunk_of(step - 4))
             products_pool(step // 2, step % 2)
             products_vector(step // 2, step % 2)
-            second_piece(chunk_of(step - 3))
-            flipped(chunk_of(step - 4))
+            flipped(chunk_of(step - 5))
             tick(n + 1)
-            exponentials(chunk_of(step - 2))
-            third_piece(chunk_of(step - 3))
             inverted(chunk_of(step - 3))
-            tick(n + 2)
-            tick(n + 3)
             scores(step // 2, step % 2)

@@ -22,7 +22,7 @@ T_POOL = 3
 PAIR = BANK // (G * CHUNK)
 BANKS_OF_CHUNK = U // PAIR
 BANKS = NCHUNK * BANKS_OF_CHUNK
-AHEAD = 2
+AHEAD = 3
 TICKS = BANKS_OF_CHUNK // G
 LAG = 8
 
@@ -186,7 +186,7 @@ def tile_localppftransformer_kernel(tc, f, nb, w_q, b_q, b_o, offs, out):
         def flipped(i):
             if not live(i):
                 return
-            flipped_ps = psum_held.tile([ROWS, G, CHUNK], BF16, name="flipped_ps")
+            flipped_ps = psum_ring.tile([ROWS, G, CHUNK], BF16, name="flipped_ps", tag="e_c")
             for g in range(G):
                 nc.tensor.transpose(
                     flipped_ps[:, g, :], of["pieces", i][:, g, :, :].rearrange("p k x -> p (k x)"), identity[:]

@@ -16,15 +16,11 @@ CHUNK = 128
 NCHUNK = N // CHUNK
 LOOK = 256
 G, U = 2, 8
-PIECES = 3
-ROWS = PIECES * H * U
-T_POOL = 3
-PAIR = BANK // (G * CHUNK)
-BANKS_OF_CHUNK = U // PAIR
-BANKS = NCHUNK * BANKS_OF_CHUNK
+T_POOL = 4
+QUAD = BANK // C
+V_BANKS = T // QUAD - 1
 AHEAD = 3
-TICKS = BANKS_OF_CHUNK // G
-LAG = 8
+LAG = 2
 
 FLOPS = 2 * C * C * N + 2 * 2 * C * T * N
 
@@ -34,10 +30,10 @@ def tile_localppftransformer_kernel(tc, f, nb, w_q, b_q, b_o, offs, out):
     with (
         tc.tile_pool(name="held", bufs=1) as held,
         tc.tile_pool(name="work", bufs=3) as work,
-        tc.tile_pool(name="soft", bufs=4) as soft,
+        tc.tile_pool(name="terms", bufs=6) as terms,
         tc.psum_pool(name="psum_held", bufs=1) as psum_held,
-        tc.psum_pool(name="psum_wide", bufs=3) as psum_wide,
-        tc.psum_pool(name="psum_ring", bufs=AHEAD + 1) as psum_ring,
+        tc.psum_pool(name="psum_sums", bufs=2) as psum_sums,
+        tc.psum_pool(name="psum_ring", bufs=AHEAD) as psum_ring,
     ):
         offsets = held.tile([C, N // 16], U16, name="offsets")
         nc.sync.dma_start(offsets[:], offs)
@@ -59,26 +55,12 @@ def tile_localppftransformer_kernel(tc, f, nb, w_q, b_q, b_o, offs, out):
         warm = held.tile([C, 1], F32, name="warm")
         nc.vector.memset(warm[:], 0.0)
         nc.scalar.activation(warm[:], warm[:], ACT.Exp)
+        identity = held.tile([C, C], F32, name="identity")
+        make_identity(nc, identity[:])
         head_of = held.tile([C, H], BF16, name="head_of")
         nc.gpsimd.memset(head_of[:], 0.0)
         for h in range(H):
             nc.gpsimd.memset(head_of[h * DH : (h + 1) * DH, h : h + 1], 1.0)
-        identity = held.tile([C, C], BF16, name="identity")
-        make_identity(nc, identity[:])
-        identity_f = held.tile([C, C], F32, name="identity_f")
-        make_identity(nc, identity_f[:])
-        pick = held.tile([C, U, H], BF16, name="pick")
-        nc.gpsimd.memset(pick[:], 0.0)
-        for piece in range(PIECES):
-            nc.gpsimd.affine_select(
-                out=pick[:], in_=pick[:], compare_op=ALU.not_equal, fill=1.0,
-                base=-H * U * piece, channel_multiplier=1, pattern=[[-1, U], [-U, H]],
-            )
-        spread = held.tile([C, U, H, DH], BF16, name="spread")
-        nc.scalar.copy(spread[:], pick[:].unsqueeze(3).to_broadcast([C, U, H, DH]))
-        e_rows = [held.tile([C, G, CHUNK], BF16, name=f"e_rows{i}") for i in range(NCHUNK)]
-        for i in range(NCHUNK):
-            nc.gpsimd.memset(e_rows[i][ROWS:C], 0.0)
 
         fn = held.tile([C, N], F32, name="fn")
         fn_bf = held.tile([C, N], BF16, name="fn_bf")
@@ -96,11 +78,17 @@ def tile_localppftransformer_kernel(tc, f, nb, w_q, b_q, b_o, offs, out):
             piece_of_list = offsets[:, k * LOOK // 16 : (k + 1) * LOOK // 16]
             nc.scalar.activation(fn[:, columns], table[:].indirect(piece_of_list), ACT.Copy)
             nc.scalar.copy(fn_bf[:, columns], fn[:, columns])
-            if k % 2 == 0:
-                of["q_bank", k // 2] = psum_wide.tile([C, BANK], F32, name="q_bank", tag="wide")
-            nc.tensor.matmul(of["q_bank", k // 2][:, (k % 2) * LOOK : (k % 2 + 1) * LOOK], wq[:], fn_bf[:, columns])
-            of["q_again", k] = psum_ring.tile([C, LOOK], F32, name="q_again", tag="e_c")
+            if k == 0:
+                query_for_vector(0)
+            of["q_again", k] = psum_ring.tile([C, LOOK], F32, name="q_again", tag="nb_t")
             nc.tensor.matmul(of["q_again", k][:], wq[:], fn_bf[:, columns])
+
+        def query_for_vector(k):
+            if k % 2 == 0:
+                of["q_bank", k // 2] = psum_held.tile([C, BANK], F32, name="q_bank")
+            columns = slice(k * LOOK, (k + 1) * LOOK)
+            half = slice(k % 2 * LOOK, (k % 2 + 1) * LOOK)
+            nc.tensor.matmul(of["q_bank", k // 2][:, half], wq[:], fn_bf[:, columns])
 
         def query_copied(k):
             nc.scalar.activation(
@@ -137,146 +125,154 @@ def tile_localppftransformer_kernel(tc, f, nb, w_q, b_q, b_o, offs, out):
             if not live(i):
                 return
             if g == 0:
-                of["score", i] = psum_held.tile([CHUNK, G, H, U], F32, name="score")
-            for u in range(U):
-                nc.tensor.matmul(of["score", i][:, g, :, u], of["prod", i][:, g * U + u, :], head_of[:])
+                of["score", i] = psum_held.tile([CHUNK, H, T], F32, name="score")
+            for t in range(g * U, (g + 1) * U):
+                nc.tensor.matmul(of["score", i][:, :, t], of["prod", i][:, t, :], head_of[:])
+
+        def largest(i):
+            if not live(i):
+                return
+            of["neg_max", i] = work.tile([CHUNK, H], F32, name="neg_max")
+            nc.vector.tensor_reduce(
+                out=of["neg_max", i][:], in_=of["score", i][:], axis=mybir.AxisListType.X, op=ALU.max, negate=True
+            )
 
         def exponentials(i):
             if not live(i):
                 return
             score = of["score", i]
-            neg_max = soft.tile([CHUNK, H], F32, name="neg_max")
-            nc.vector.tensor_reduce(
-                out=neg_max[:], in_=score[:].rearrange("p g h u -> p h g u"),
-                axis=mybir.AxisListType.XY, op=ALU.max, negate=True,
-            )
-            shift = soft.tile([CHUNK, H], F32, name="shift")
-            nc.scalar.mul(shift[:], neg_max[:], SCALE)
-            e = soft.tile([CHUNK, G, H, U], F32, name="e")
-            of["total", i] = soft.tile([CHUNK, H], F32, name="total")
+            shift = work.tile([CHUNK, H], F32, name="shift")
+            nc.scalar.mul(shift[:], of["neg_max", i][:], SCALE)
+            of["e", i] = work.tile([CHUNK, H, T], F32, name="e")
+            of["total", i] = work.tile([CHUNK, H], F32, name="total")
             for h in range(H):
                 nc.scalar.activation(
-                    e[:, :, h, :], score[:, :, h, :], ACT.Exp,
+                    of["e", i][:, h, :], score[:, h, :], ACT.Exp,
                     bias=shift[:, h : h + 1], scale=SCALE, accum_out=of["total", i][:, h : h + 1],
                 )
-            of["e", i] = e[:].rearrange("p g h u -> p g (h u)")
-            of["pieces", i] = soft.tile([CHUNK, G, PIECES, H * U], BF16, name="pieces")
-            nc.scalar.copy(of["pieces", i][:, :, 0, :], of["e", i])
 
-        def inverted(i):
+        def weights(i):
             if not live(i):
                 return
-            of["inverse", i] = held.tile([CHUNK, H], F32, name=f"inverse{i}")
-            nc.vector.reciprocal(of["inverse", i][:], of["total", i][:])
-
-        def second_piece(i):
-            if not live(i):
-                return
-            of["rest", i] = soft.tile([CHUNK, G, H * U], F32, name="rest")
-            nc.gpsimd.tensor_tensor(of["rest", i][:], of["e", i], of["pieces", i][:, :, 0, :], ALU.subtract)
-            nc.scalar.copy(of["pieces", i][:, :, 1, :], of["rest", i][:])
-
-        def third_piece(i):
-            if not live(i):
-                return
-            nc.gpsimd.tensor_tensor(
-                of["pieces", i][:, :, 2, :], of["rest", i][:], of["pieces", i][:, :, 1, :], ALU.subtract
-            )
-
-        def flipped(i):
-            if not live(i):
-                return
-            flipped_ps = psum_ring.tile([ROWS, G, CHUNK], BF16, name="flipped_ps", tag="e_c")
-            for g in range(G):
-                nc.tensor.transpose(
-                    flipped_ps[:, g, :], of["pieces", i][:, g, :, :].rearrange("p k x -> p (k x)"), identity[:]
-                )
-            nc.scalar.copy(e_rows[i][0:ROWS], flipped_ps[:])
-
-        def spread_out(n):
-            if not 0 <= n < BANKS:
-                return
-            i, k = divmod(n, BANKS_OF_CHUNK)
-            of["e_c", n] = psum_ring.tile([C, PAIR, G, CHUNK], F32, name="e_c")
-            for v in range(PAIR):
-                nc.tensor.matmul(
-                    of["e_c", n][:, v].rearrange("c g j -> c (g j)"),
-                    spread[:, PAIR * k + v, :, :].rearrange("r h d -> r (h d)"),
-                    e_rows[i][:].rearrange("r g j -> r (g j)"),
-                )
-
-        def multiplied(n):
-            if not 0 <= n < BANKS:
-                return
-            i, k = divmod(n, BANKS_OF_CHUNK)
-            if k == 0:
-                of["terms", i] = work.tile([C, U, G, CHUNK], F32, name="terms")
-            us = slice(PAIR * k, PAIR * (k + 1))
-            nc.vector.tensor_tensor(
-                of["terms", i][:, us], of["e_c", n][:], nbr[i][:].rearrange("c (g u) j -> c u g j", g=G)[:, us], ALU.mult
-            )
-
-        def added(n):
-            if not 0 <= n < BANKS:
-                return
-            i, k = divmod(n, BANKS_OF_CHUNK)
-            if k == 0:
-                of["sums", i] = psum_wide.tile([C, 2, CHUNK], F32, name="sums", tag="wide")
-            for u in range(PAIR * k, PAIR * (k + 1)):
-                for g in range(G):
-                    nc.tensor.matmul(
-                        of["sums", i][:, 0, :], of["terms", i][:, u, g, :], identity_f[:],
-                        start=(u == 0 and g == 0), stop=(u == U - 1 and g == G - 1), is_transpose=True,
-                    )
-
-        def copied_out(i):
-            if not live(i):
-                return
-            of["sum_sbuf", i] = work.tile([CHUNK, C], F32, name="sum_sbuf")
+            inverse = work.tile([CHUNK, H], F32, name="inverse")
+            nc.vector.reciprocal(inverse[:], of["total", i][:])
+            of["attn", i] = work.tile([CHUNK, H, T], F32, name="attn")
             for h in range(H):
                 nc.scalar.activation(
-                    of["sum_sbuf", i][:, h * DH : (h + 1) * DH], of["sums", i][:, 0, h * DH : (h + 1) * DH],
-                    ACT.Copy, scale=of["inverse", i][:, h : h + 1],
+                    of["attn", i][:, h, :], of["e", i][:, h, :], ACT.Copy, scale=inverse[:, h : h + 1]
+                )
+
+        def turned(i, quad, pool, name):
+            nb_t = pool.tile([CHUNK, QUAD, C], F32, name=name)
+            for v in range(QUAD):
+                nc.tensor.transpose(nb_t[:, v, :], nbr[i][:, quad * QUAD + v, :], identity[:])
+            return nb_t
+
+        def turned_for_vector(n):
+            if 0 <= n < NCHUNK * V_BANKS:
+                of["nb_t", n] = turned(n // V_BANKS, n % V_BANKS, psum_ring, "nb_t")
+
+        def turned_for_scalar(i):
+            if live(i):
+                of["nb_s", i] = turned(i, V_BANKS, psum_held, "nb_s")
+
+        def terms_vector(n):
+            if not 0 <= n < NCHUNK * V_BANKS:
+                return
+            i, quad = divmod(n, V_BANKS)
+            of["terms", n] = terms.tile([CHUNK, QUAD, H, DH], F32, name="terms")
+            attn = of["attn", i][:, :, quad * QUAD : (quad + 1) * QUAD].rearrange("p h t -> p t h")
+            nc.vector.tensor_tensor(
+                of["terms", n][:],
+                of["nb_t", n][:].rearrange("p t (h d) -> p t h d", h=H),
+                attn.unsqueeze(3).to_broadcast([CHUNK, QUAD, H, DH]),
+                ALU.mult,
+            )
+
+        def terms_scalar(i, half):
+            if not live(i):
+                return
+            if half == 0:
+                of["terms_s", i] = work.tile([CHUNK, QUAD, C], F32, name="terms_s")
+            for v in range(half * QUAD // 2, (half + 1) * QUAD // 2):
+                t = V_BANKS * QUAD + v
+                for h in range(H):
+                    head = slice(h * DH, (h + 1) * DH)
+                    nc.scalar.activation(
+                        of["terms_s", i][:, v, head], of["nb_s", i][:, v, head], ACT.Copy,
+                        scale=of["attn", i][:, h, t : t + 1],
+                    )
+
+        def added_vector(n):
+            if not 0 <= n < NCHUNK * V_BANKS:
+                return
+            i, quad = divmod(n, V_BANKS)
+            if quad == 0:
+                of["sums", i] = psum_sums.tile([C, CHUNK], F32, name="sums")
+                nc.tensor.matmul(of["sums", i][:], identity[:], fn[:, columns_of(i)], start=True, stop=False)
+            for v in range(QUAD):
+                nc.tensor.matmul(
+                    of["sums", i][:], of["terms", n][:, v].rearrange("p h d -> p (h d)"), identity[:],
+                    start=False, stop=False, is_transpose=True,
+                )
+
+        def added_scalar(i):
+            if not live(i):
+                return
+            for v in range(QUAD):
+                nc.tensor.matmul(
+                    of["sums", i][:], of["terms_s", i][:, v, :], identity[:],
+                    start=False, stop=(v == QUAD - 1), is_transpose=True,
                 )
 
         def finished(i):
             if not live(i):
                 return
-            nc.tensor.matmul(of["sums", i][:, 1, :], identity_f[:], fn[:, columns_of(i)], start=True, stop=False)
-            nc.tensor.matmul(
-                of["sums", i][:, 1, :], of["sum_sbuf", i][:], identity_f[:], start=False, stop=True, is_transpose=True
-            )
             result = work.tile([C, CHUNK], F32, name="result")
-            nc.scalar.activation(result[:], of["sums", i][:, 1, :], ACT.Identity, bias=bo[:, 0:1])
+            nc.scalar.activation(result[:], of["sums", i][:], ACT.Identity, bias=bo[:, 0:1])
             nc.sync.dma_start(out[:, columns_of(i)], result[:])
 
         looked_up(0)
         for k in range(1, N // LOOK):
             looked_up(k)
             query_copied(k - 1)
+            if k == 1:
+                query_for_vector(1)
         query_copied(N // LOOK - 1)
-
-        def chunk_of(step):
-            return step // 2 if step % 2 == 0 else -1
+        for n in range(AHEAD):
+            turned_for_vector(n)
 
         def tick(n):
-            multiplied(n)
-            spread_out(n + AHEAD)
-            added(n - 1)
-            if n % BANKS_OF_CHUNK == 0:
-                copied_out(n // BANKS_OF_CHUNK - 1)
-            if n % BANKS_OF_CHUNK == 2:
-                finished(n // BANKS_OF_CHUNK - 1)
+            terms_vector(n)
+            turned_for_vector(n + AHEAD)
+            added_vector(n - 1)
 
-        for step in range(G * NCHUNK + LAG + 2):
-            n = TICKS * (step - LAG)
-            tick(n)
-            exponentials(chunk_of(step - 2))
-            second_piece(chunk_of(step - 3))
-            third_piece(chunk_of(step - 4))
-            products_pool(step // 2, step % 2)
-            products_vector(step // 2, step % 2)
-            flipped(chunk_of(step - 5))
-            tick(n + 1)
-            inverted(chunk_of(step - 3))
-            scores(step // 2, step % 2)
+        for i in range(NCHUNK + LAG + 1):
+            late = i - LAG
+            n = late * V_BANKS
+            largest(i - 1)
+            exponentials(i - 1)
+            products_pool(i, 0)
+            products_vector(i, 0)
+            turned_for_vector(n + AHEAD)
+            turned_for_scalar(late)
+            added_vector(n)
+            terms_vector(n + 1)
+            scores(i, 0)
+            turned_for_vector(n + 1 + AHEAD)
+            terms_scalar(late, 0)
+            weights(i - 1)
+            terms_scalar(late, 1)
+            finished(late - 1)
+            products_pool(i, 1)
+            products_vector(i, 1)
+            added_vector(n + 1)
+            if i == BANK // CHUNK - 1:
+                query_for_vector(2)
+                query_for_vector(3)
+            terms_vector(n + 2)
+            scores(i, 1)
+            turned_for_vector(n + 2 + AHEAD)
+            terms_vector(n + 3)
+            added_vector(n + 2)
+            added_scalar(late)

@@ -14,7 +14,6 @@ SCALE = 1.0 / math.sqrt(DH)
 BANK = 512
 CHUNK = 128
 NCHUNK = N // CHUNK
-LOOK = 256
 G, U = 2, 8
 T_POOL = 4
 QUAD = BANK // C
@@ -73,33 +72,37 @@ def tile_localppftransformer_kernel(tc, f, nb, w_q, b_q, b_o, offs, out):
         def columns_of(i):
             return slice(i * CHUNK, (i + 1) * CHUNK)
 
-        def looked_up(k):
-            columns = slice(k * LOOK, (k + 1) * LOOK)
-            piece_of_list = offsets[:, k * LOOK // 16 : (k + 1) * LOOK // 16]
-            nc.scalar.activation(fn[:, columns], table[:].indirect(piece_of_list), ACT.Copy)
-            nc.scalar.copy(fn_bf[:, columns], fn[:, columns])
-            if k == 0:
-                query_for_vector(0)
-            of["q_again", k] = psum_ring.tile([C, LOOK], F32, name="q_again", tag="nb_t")
-            nc.tensor.matmul(of["q_again", k][:], wq[:], fn_bf[:, columns])
+        def looked_up(i):
+            piece_of_list = offsets[:, i * CHUNK // 16 : (i + 1) * CHUNK // 16]
+            nc.scalar.activation(fn[:, columns_of(i)], table[:].indirect(piece_of_list), ACT.Copy)
 
-        def query_for_vector(k):
-            if k % 2 == 0:
-                of["q_bank", k // 2] = psum_held.tile([C, BANK], F32, name="q_bank")
-            columns = slice(k * LOOK, (k + 1) * LOOK)
-            half = slice(k % 2 * LOOK, (k % 2 + 1) * LOOK)
-            nc.tensor.matmul(of["q_bank", k // 2][:, half], wq[:], fn_bf[:, columns])
+        def rounded(i):
+            nc.scalar.copy(fn_bf[:, columns_of(i)], fn[:, columns_of(i)])
 
-        def query_copied(k):
-            nc.scalar.activation(
-                q_sbuf[:, k * LOOK : (k + 1) * LOOK], of["q_again", k][:], ACT.Identity, bias=bq[:, 0:1]
-            )
+        def query_for_vector(i):
+            if i == 0:
+                q_first = psum_ring.tile([C, CHUNK], F32, name="q_first", tag="nb_t")
+                of["q", 0] = q_first[:]
+            else:
+                if i == 1 or i * CHUNK % BANK == 0:
+                    of["q_bank"] = psum_held.tile([C, BANK], F32, name="q_bank")
+                of["q", i] = of["q_bank"][:, i * CHUNK % BANK : i * CHUNK % BANK + CHUNK]
+            nc.tensor.matmul(of["q", i], wq[:], fn_bf[:, columns_of(i)])
+
+        def query_for_pool(i):
+            of["q_again", i] = psum_sums.tile([C, CHUNK], F32, name="q_again", tag="sums")
+            nc.tensor.matmul(of["q_again", i][:], wq[:], fn_bf[:, columns_of(i)])
+
+        def query_copied(i):
+            nc.scalar.activation(q_sbuf[:, columns_of(i)], of["q_again", i][:], ACT.Identity, bias=bq[:, 0:1])
 
         def products_pool(i, g):
             if not live(i):
                 return
             if g == 0:
                 of["prod", i] = work.tile([C, T, CHUNK], BF16, name="prod")
+            if i < 1:
+                return
             lo = g * U
             nc.gpsimd.tensor_tensor(
                 of["prod", i][:, lo : lo + T_POOL, :],
@@ -111,11 +114,10 @@ def tile_localppftransformer_kernel(tc, f, nb, w_q, b_q, b_o, offs, out):
         def products_vector(i, g):
             if not live(i):
                 return
-            lo, hi = g * U + T_POOL, (g + 1) * U
-            at = i * CHUNK % BANK
+            lo, hi = g * U + (T_POOL if i >= 1 else 0), (g + 1) * U
             nc.vector.scalar_tensor_tensor(
                 out=of["prod", i][:, lo:hi, :],
-                in0=of["q_bank", i * CHUNK // BANK][:, at : at + CHUNK].unsqueeze(1).to_broadcast([C, hi - lo, CHUNK]),
+                in0=of["q", i].unsqueeze(1).to_broadcast([C, hi - lo, CHUNK]),
                 scalar=bq[:, 0:1],
                 in1=nbr[i][:, lo:hi, :],
                 op0=ALU.add, op1=ALU.mult,
@@ -232,26 +234,31 @@ def tile_localppftransformer_kernel(tc, f, nb, w_q, b_q, b_o, offs, out):
             nc.scalar.activation(result[:], of["sums", i][:], ACT.Identity, bias=bo[:, 0:1])
             nc.sync.dma_start(out[:, columns_of(i)], result[:])
 
+        FIRST = BANK // CHUNK
         looked_up(0)
-        for k in range(1, N // LOOK):
-            looked_up(k)
-            query_copied(k - 1)
-            if k == 1:
-                query_for_vector(1)
-        query_copied(N // LOOK - 1)
-        for n in range(AHEAD):
-            turned_for_vector(n)
-
-        def tick(n):
-            terms_vector(n)
-            turned_for_vector(n + AHEAD)
-            added_vector(n - 1)
+        for i in range(FIRST):
+            if i + 1 < FIRST:
+                looked_up(i + 1)
+            rounded(i)
+            query_for_vector(i)
+            if i == 0:
+                turned_for_vector(0)
+                turned_for_vector(1)
+            else:
+                query_for_pool(i)
+                query_copied(i)
 
         for i in range(NCHUNK + LAG + 1):
             late = i - LAG
             n = late * V_BANKS
             largest(i - 1)
             exponentials(i - 1)
+            if i < FIRST // 2:
+                for k in range(FIRST + 2 * i, FIRST + 2 * i + 2):
+                    looked_up(k)
+                    rounded(k)
+                    query_for_pool(k)
+                    query_copied(k)
             products_pool(i, 0)
             products_vector(i, 0)
             turned_for_vector(n + AHEAD)
@@ -259,6 +266,8 @@ def tile_localppftransformer_kernel(tc, f, nb, w_q, b_q, b_o, offs, out):
             added_vector(n)
             terms_vector(n + 1)
             scores(i, 0)
+            if i == 0:
+                turned_for_vector(2)
             turned_for_vector(n + 1 + AHEAD)
             terms_scalar(late, 0)
             weights(i - 1)
@@ -267,9 +276,9 @@ def tile_localppftransformer_kernel(tc, f, nb, w_q, b_q, b_o, offs, out):
             products_pool(i, 1)
             products_vector(i, 1)
             added_vector(n + 1)
-            if i == BANK // CHUNK - 1:
-                query_for_vector(2)
-                query_for_vector(3)
+            if i == FIRST - 1:
+                for k in range(FIRST, NCHUNK):
+                    query_for_vector(k)
             terms_vector(n + 2)
             scores(i, 1)
             turned_for_vector(n + 2 + AHEAD)

@@ -211,11 +211,10 @@ def tile_localppftransformer_kernel(tc, f, nb, w_q, b_q, b_o, offs, out):
             i, quad = divmod(n, V_BANKS)
             if quad == 0:
                 of["sums", i] = psum_sums.tile([C, CHUNK], F32, name="sums")
-                nc.tensor.matmul(of["sums", i][:], identity[:], fn[:, columns_of(i)], start=True, stop=False)
             for v in range(QUAD):
                 nc.tensor.matmul(
                     of["sums", i][:], of["terms", n][:, v].rearrange("p h d -> p (h d)"), identity[:],
-                    start=False, stop=False, is_transpose=True,
+                    start=(quad == 0 and v == 0), stop=False, is_transpose=True,
                 )
 
         def added_scalar(i):
@@ -231,7 +230,9 @@ def tile_localppftransformer_kernel(tc, f, nb, w_q, b_q, b_o, offs, out):
             if not live(i):
                 return
             result = work.tile([C, CHUNK], F32, name="result")
-            nc.scalar.activation(result[:], of["sums", i][:], ACT.Identity, bias=bo[:, 0:1])
+            nc.vector.scalar_tensor_tensor(
+                out=result[:], in0=of["sums", i][:], scalar=bo[:, 0:1], in1=fn[:, columns_of(i)], op0=ALU.add, op1=ALU.add
+            )
             nc.sync.dma_start(out[:, columns_of(i)], result[:])
 
         FIRST = BANK // CHUNK

@@ -11,6 +11,7 @@ C, S, N, T, H = 128, 4096, 1024, 16, 4
 DH = C // H
 SCALE = 1.0 / math.sqrt(DH)
 
+SCORE_COLUMNS = 32
 BANK = 512
 CHUNK = 128
 NCHUNK = N // CHUNK
@@ -56,7 +57,7 @@ def tile_localppftransformer_kernel(tc, f, nb, w_q, b_q, b_o, offs, out):
         nc.scalar.activation(warm[:], warm[:], ACT.Exp)
         identity = held.tile([C, C], F32, name="identity")
         make_identity(nc, identity[:])
-        head_of = held.tile([C, H], BF16, name="head_of")
+        head_of = held.tile([C, SCORE_COLUMNS], BF16, name="head_of")
         nc.gpsimd.memset(head_of[:], 0.0)
         for h in range(H):
             nc.gpsimd.memset(head_of[h * DH : (h + 1) * DH, h : h + 1], 1.0)
@@ -127,7 +128,7 @@ def tile_localppftransformer_kernel(tc, f, nb, w_q, b_q, b_o, offs, out):
             if not live(i):
                 return
             if g == 0:
-                of["score", i] = psum_held.tile([CHUNK, H, T], F32, name="score")
+                of["score", i] = psum_held.tile([CHUNK, SCORE_COLUMNS, T], F32, name="score")
             for t in range(g * U, (g + 1) * U):
                 nc.tensor.matmul(of["score", i][:, :, t], of["prod", i][:, t, :], head_of[:])
 
@@ -136,7 +137,7 @@ def tile_localppftransformer_kernel(tc, f, nb, w_q, b_q, b_o, offs, out):
                 return
             of["neg_max", i] = work.tile([CHUNK, H], F32, name="neg_max")
             nc.vector.tensor_reduce(
-                out=of["neg_max", i][:], in_=of["score", i][:], axis=mybir.AxisListType.X, op=ALU.max, negate=True
+                out=of["neg_max", i][:], in_=of["score", i][:, 0:H, :], axis=mybir.AxisListType.X, op=ALU.max, negate=True
             )
 
         def exponentials(i):
@@ -242,10 +243,7 @@ def tile_localppftransformer_kernel(tc, f, nb, w_q, b_q, b_o, offs, out):
                 looked_up(i + 1)
             rounded(i)
             query_for_vector(i)
-            if i == 0:
-                turned_for_vector(0)
-                turned_for_vector(1)
-            else:
+            if i > 0:
                 query_for_pool(i)
                 query_copied(i)
 
@@ -254,12 +252,6 @@ def tile_localppftransformer_kernel(tc, f, nb, w_q, b_q, b_o, offs, out):
             n = late * V_BANKS
             largest(i - 1)
             exponentials(i - 1)
-            if i < FIRST // 2:
-                for k in range(FIRST + 2 * i, FIRST + 2 * i + 2):
-                    looked_up(k)
-                    rounded(k)
-                    query_for_pool(k)
-                    query_copied(k)
             products_pool(i, 0)
             products_vector(i, 0)
             turned_for_vector(n + AHEAD)
@@ -267,8 +259,6 @@ def tile_localppftransformer_kernel(tc, f, nb, w_q, b_q, b_o, offs, out):
             added_vector(n)
             terms_vector(n + 1)
             scores(i, 0)
-            if i == 0:
-                turned_for_vector(2)
             turned_for_vector(n + 1 + AHEAD)
             terms_scalar(late, 0)
             weights(i - 1)
@@ -282,6 +272,12 @@ def tile_localppftransformer_kernel(tc, f, nb, w_q, b_q, b_o, offs, out):
                     query_for_vector(k)
             terms_vector(n + 2)
             scores(i, 1)
+            if i < FIRST // 2:
+                for k in range(FIRST + 2 * i, FIRST + 2 * i + 2):
+                    looked_up(k)
+                    rounded(k)
+                    query_for_pool(k)
+                    query_copied(k)
             turned_for_vector(n + 2 + AHEAD)
             terms_vector(n + 3)
             added_vector(n + 2)

@@ -32,13 +32,13 @@ def tile_localppftransformer_kernel(tc, f, nb, w_q, b_q, b_o, offs, out):
         tc.tile_pool(name="work", bufs=3) as work,
         tc.tile_pool(name="terms", bufs=6) as terms,
         tc.psum_pool(name="psum_held", bufs=1) as psum_held,
-        tc.psum_pool(name="psum_sums", bufs=2) as psum_sums,
+        tc.psum_pool(name="psum_sums", bufs=3) as psum_sums,
         tc.psum_pool(name="psum_ring", bufs=AHEAD) as psum_ring,
     ):
         offsets = held.tile([C, N // 16], U16, name="offsets")
-        nc.sync.dma_start(offsets[:], offs)
         table = held.tile([C, S], F32, name="table")
         nc.sync.dma_start(table[:], f)
+        nc.sync.dma_start(offsets[:], offs)
         nbr = [held.tile([C, T, CHUNK], F32, name=f"nbr{i}") for i in range(NCHUNK)]
         for i in range(NCHUNK):
             for g in range(G):
@@ -78,11 +78,14 @@ def tile_localppftransformer_kernel(tc, f, nb, w_q, b_q, b_o, offs, out):
             nc.scalar.activation(fn[:, columns_of(i)], table[:].indirect(piece_of_list), ACT.Copy)
 
         def rounded(i):
-            nc.scalar.copy(fn_bf[:, columns_of(i)], fn[:, columns_of(i)])
+            if i == 0:
+                nc.vector.tensor_copy(fn_bf[:, columns_of(i)], fn[:, columns_of(i)])
+            else:
+                nc.scalar.copy(fn_bf[:, columns_of(i)], fn[:, columns_of(i)])
 
         def query_for_vector(i):
             if i == 0:
-                q_first = psum_ring.tile([C, CHUNK], F32, name="q_first", tag="nb_t")
+                q_first = psum_held.tile([C, CHUNK], F32, name="q_first", tag="nb_s")
                 of["q", 0] = q_first[:]
             else:
                 if i == 1 or i * CHUNK % BANK == 0:
@@ -128,7 +131,7 @@ def tile_localppftransformer_kernel(tc, f, nb, w_q, b_q, b_o, offs, out):
             if not live(i):
                 return
             if g == 0:
-                of["score", i] = psum_held.tile([CHUNK, SCORE_COLUMNS, T], F32, name="score")
+                of["score", i] = psum_sums.tile([CHUNK, SCORE_COLUMNS, T], F32, name="score", tag="sums")
             for t in range(g * U, (g + 1) * U):
                 nc.tensor.matmul(of["score", i][:, :, t], of["prod", i][:, t, :], head_of[:])
 
@@ -243,7 +246,10 @@ def tile_localppftransformer_kernel(tc, f, nb, w_q, b_q, b_o, offs, out):
                 looked_up(i + 1)
             rounded(i)
             query_for_vector(i)
-            if i > 0:
+            if i == 0:
+                for n in range(AHEAD):
+                    turned_for_vector(n)
+            else:
                 query_for_pool(i)
                 query_copied(i)
 
@@ -254,12 +260,12 @@ def tile_localppftransformer_kernel(tc, f, nb, w_q, b_q, b_o, offs, out):
             exponentials(i - 1)
             products_pool(i, 0)
             products_vector(i, 0)
-            turned_for_vector(n + AHEAD)
-            turned_for_scalar(late)
+            if late >= 0:
+                turned_for_vector(n + AHEAD)
             added_vector(n)
             terms_vector(n + 1)
-            scores(i, 0)
-            turned_for_vector(n + 1 + AHEAD)
+            if late >= 0:
+                turned_for_vector(n + 1 + AHEAD)
             terms_scalar(late, 0)
             weights(i - 1)
             terms_scalar(late, 1)
@@ -271,14 +277,17 @@ def tile_localppftransformer_kernel(tc, f, nb, w_q, b_q, b_o, offs, out):
                 for k in range(FIRST, NCHUNK):
                     query_for_vector(k)
             terms_vector(n + 2)
+            scores(i, 0)
             scores(i, 1)
-            if i < FIRST // 2:
-                for k in range(FIRST + 2 * i, FIRST + 2 * i + 2):
+            if 0 < i <= FIRST // 2:
+                for k in range(FIRST + 2 * i - 2, FIRST + 2 * i):
                     looked_up(k)
                     rounded(k)
                     query_for_pool(k)
                     query_copied(k)
-            turned_for_vector(n + 2 + AHEAD)
+            if late >= 0:
+                turned_for_vector(n + 2 + AHEAD)
             terms_vector(n + 3)
+            turned_for_scalar(late + 1)
             added_vector(n + 2)
             added_scalar(late)

import math

import concourse.mybir as mybir
from concourse.masks import make_identity

F32, BF16, U16 = mybir.dt.float32, mybir.dt.bfloat16, mybir.dt.uint16
ALU = mybir.AluOpType
ACT = mybir.ActivationFunctionType

C, S, N, T, H = 128, 4096, 1024, 16, 4
DH = C // H
SCALE = 1.0 / math.sqrt(DH)

SCORE_COLUMNS = 32
BANK = 512
CHUNK = 128
NCHUNK = N // CHUNK
G, U = 2, 8
T_POOL = 4
QUAD = BANK // C
V_BANKS = T // QUAD - 1
AHEAD = 3
LAG = 2

FLOPS = 2 * C * C * N + 2 * 2 * C * T * N


def tile_localppftransformer_kernel(tc, f, nb, w_q, b_q, b_o, offs, out):
    nc = tc.nc
    with (
        tc.tile_pool(name="held", bufs=1) as held,
        tc.tile_pool(name="work", bufs=3) as work,
        tc.tile_pool(name="terms", bufs=6) as terms,
        tc.psum_pool(name="psum_held", bufs=1) as psum_held,
        tc.psum_pool(name="psum_sums", bufs=3) as psum_sums,
        tc.psum_pool(name="psum_ring", bufs=AHEAD) as psum_ring,
    ):
        offsets = held.tile([C, N // 16], U16, name="offsets")
        table = held.tile([C, S], F32, name="table")
        nc.sync.dma_start(table[:], f)
        nc.sync.dma_start(offsets[:], offs)
        nbr = [held.tile([C, T, CHUNK], F32, name=f"nbr{i}") for i in range(NCHUNK)]
        for i in range(NCHUNK):
            for g in range(G):
                nc.sync.dma_start(
                    nbr[i][:, g * U : (g + 1) * U, :], nb[:, g * U : (g + 1) * U, i * CHUNK : (i + 1) * CHUNK]
                )
        wq = held.tile([C, C], BF16, name="wq")
        nc.scalar.dma_start(wq[:], w_q)
        bq = held.tile([C, 1], F32, name="bq")
        nc.scalar.dma_start(bq[:], b_q)
        bo = held.tile([C, 1], F32, name="bo")
        nc.scalar.dma_start(bo[:], b_o)

        warm = held.tile([C, 1], F32, name="warm")
        nc.vector.memset(warm[:], 0.0)
        nc.scalar.activation(warm[:], warm[:], ACT.Exp)
        identity = held.tile([C, C], F32, name="identity")
        make_identity(nc, identity[:])
        head_of = held.tile([C, SCORE_COLUMNS], BF16, name="head_of")
        nc.gpsimd.memset(head_of[:], 0.0)
        for h in range(H):
            nc.gpsimd.memset(head_of[h * DH : (h + 1) * DH, h : h + 1], 1.0)

        fn = held.tile([C, N], F32, name="fn")
        fn_bf = held.tile([C, N], BF16, name="fn_bf")
        q_sbuf = held.tile([C, N], F32, name="q_sbuf")
        of = {}

        def live(i):
            return 0 <= i < NCHUNK

        def columns_of(i):
            return slice(i * CHUNK, (i + 1) * CHUNK)

        def looked_up(i):
            piece_of_list = offsets[:, i * CHUNK // 16 : (i + 1) * CHUNK // 16]
            nc.scalar.activation(fn[:, columns_of(i)], table[:].indirect(piece_of_list), ACT.Copy)

        def rounded(i):
            if i == 0:
                nc.vector.tensor_copy(fn_bf[:, columns_of(i)], fn[:, columns_of(i)])
            else:
                nc.scalar.copy(fn_bf[:, columns_of(i)], fn[:, columns_of(i)])

        def query_for_vector(i):
            if i == 0:
                q_first = psum_held.tile([C, CHUNK], F32, name="q_first", tag="nb_s")
                of["q", 0] = q_first[:]
            else:
                if i == 1 or i * CHUNK % BANK == 0:
                    of["q_bank"] = psum_held.tile([C, BANK], F32, name="q_bank")
                of["q", i] = of["q_bank"][:, i * CHUNK % BANK : i * CHUNK % BANK + CHUNK]
            nc.tensor.matmul(of["q", i], wq[:], fn_bf[:, columns_of(i)])

        def query_for_pool(i):
            of["q_again", i] = psum_sums.tile([C, CHUNK], F32, name="q_again", tag="sums")
            nc.tensor.matmul(of["q_again", i][:], wq[:], fn_bf[:, columns_of(i)])

        def query_copied(i):
            nc.scalar.activation(q_sbuf[:, columns_of(i)], of["q_again", i][:], ACT.Identity, bias=bq[:, 0:1])

        def products_pool(i, g):
            if not live(i):
                return
            if g == 0:
                of["prod", i] = work.tile([C, T, CHUNK], BF16, name="prod")
            if i < 1:
                return
            lo = g * U
            nc.gpsimd.tensor_tensor(
                of["prod", i][:, lo : lo + T_POOL, :],
                q_sbuf[:, columns_of(i)].unsqueeze(1).to_broadcast([C, T_POOL, CHUNK]),
                nbr[i][:, lo : lo + T_POOL, :],
                ALU.mult,
            )

        def products_vector(i, g):
            if not live(i):
                return
            lo, hi = g * U + (T_POOL if i >= 1 else 0), (g + 1) * U
            nc.vector.scalar_tensor_tensor(
                out=of["prod", i][:, lo:hi, :],
                in0=of["q", i].unsqueeze(1).to_broadcast([C, hi - lo, CHUNK]),
                scalar=bq[:, 0:1],
                in1=nbr[i][:, lo:hi, :],
                op0=ALU.add, op1=ALU.mult,
            )

        def scores(i, g):
            if not live(i):
                return
            if g == 0:
                of["score", i] = psum_sums.tile([CHUNK, SCORE_COLUMNS, T], F32, name="score", tag="sums")
            for t in range(g * U, (g + 1) * U):
                nc.tensor.matmul(of["score", i][:, :, t], of["prod", i][:, t, :], head_of[:])

        def largest(i):
            if not live(i):
                return
            of["neg_max", i] = work.tile([CHUNK, H], F32, name="neg_max")
            nc.vector.tensor_reduce(
                out=of["neg_max", i][:], in_=of["score", i][:, 0:H, :], axis=mybir.AxisListType.X, op=ALU.max, negate=True
            )

        def exponentials(i):
            if not live(i):
                return
            score = of["score", i]
            shift = work.tile([CHUNK, H], F32, name="shift")
            nc.scalar.mul(shift[:], of["neg_max", i][:], SCALE)
            of["e", i] = work.tile([CHUNK, H, T], F32, name="e")
            of["total", i] = work.tile([CHUNK, H], F32, name="total")
            for h in range(H):
                nc.scalar.activation(
                    of["e", i][:, h, :], score[:, h, :], ACT.Exp,
                    bias=shift[:, h : h + 1], scale=SCALE, accum_out=of["total", i][:, h : h + 1],
                )

        def weights(i):
            if not live(i):
                return
            inverse = work.tile([CHUNK, H], F32, name="inverse")
            nc.vector.reciprocal(inverse[:], of["total", i][:])
            of["attn", i] = work.tile([CHUNK, H, T], F32, name="attn")
            for h in range(H):
                nc.scalar.activation(
                    of["attn", i][:, h, :], of["e", i][:, h, :], ACT.Copy, scale=inverse[:, h : h + 1]
                )

        def turned(i, quad, pool, name):
            nb_t = pool.tile([CHUNK, QUAD, C], F32, name=name)
            for v in range(QUAD):
                nc.tensor.transpose(nb_t[:, v, :], nbr[i][:, quad * QUAD + v, :], identity[:])
            return nb_t

        def turned_for_vector(n):
            if 0 <= n < NCHUNK * V_BANKS:
                of["nb_t", n] = turned(n // V_BANKS, n % V_BANKS, psum_ring, "nb_t")

        def turned_for_scalar(i):
            if live(i):
                of["nb_s", i] = turned(i, V_BANKS, psum_held, "nb_s")

        def terms_vector(n):
            if not 0 <= n < NCHUNK * V_BANKS:
                return
            i, quad = divmod(n, V_BANKS)
            of["terms", n] = terms.tile([CHUNK, QUAD, H, DH], F32, name="terms")
            attn = of["attn", i][:, :, quad * QUAD : (quad + 1) * QUAD].rearrange("p h t -> p t h")
            nc.vector.tensor_tensor(
                of["terms", n][:],
                of["nb_t", n][:].rearrange("p t (h d) -> p t h d", h=H),
                attn.unsqueeze(3).to_broadcast([CHUNK, QUAD, H, DH]),
                ALU.mult,
            )

        def terms_scalar(i, half):
            if not live(i):
                return
            if half == 0:
                of["terms_s", i] = work.tile([CHUNK, QUAD, C], F32, name="terms_s")
            for v in range(half * QUAD // 2, (half + 1) * QUAD // 2):
                t = V_BANKS * QUAD + v
                for h in range(H):
                    head = slice(h * DH, (h + 1) * DH)
                    nc.scalar.activation(
                        of["terms_s", i][:, v, head], of["nb_s", i][:, v, head], ACT.Copy,
                        scale=of["attn", i][:, h, t : t + 1],
                    )

        def added_vector(n):
            if not 0 <= n < NCHUNK * V_BANKS:
                return
            i, quad = divmod(n, V_BANKS)
            if quad == 0:
                of["sums", i] = psum_sums.tile([C, CHUNK], F32, name="sums")
            for v in range(QUAD):
                nc.tensor.matmul(
                    of["sums", i][:], of["terms", n][:, v].rearrange("p h d -> p (h d)"), identity[:],
                    start=(quad == 0 and v == 0), stop=False, is_transpose=True,
                )

        def added_scalar(i):
            if not live(i):
                return
            for v in range(QUAD):
                nc.tensor.matmul(
                    of["sums", i][:], of["terms_s", i][:, v, :], identity[:],
                    start=False, stop=(v == QUAD - 1), is_transpose=True,
                )

        def finished(i):
            if not live(i):
                return
            result = work.tile([C, CHUNK], F32, name="result")
            nc.vector.scalar_tensor_tensor(
                out=result[:], in0=of["sums", i][:], scalar=bo[:, 0:1], in1=fn[:, columns_of(i)], op0=ALU.add, op1=ALU.add
            )
            nc.sync.dma_start(out[:, columns_of(i)], result[:])

        FIRST = BANK // CHUNK
        looked_up(0)
        for i in range(FIRST):
            if i + 1 < FIRST:
                looked_up(i + 1)
            rounded(i)
            query_for_vector(i)
            if i == 0:
                for n in range(AHEAD):
                    turned_for_vector(n)
            else:
                query_for_pool(i)
                query_copied(i)

        for i in range(NCHUNK + LAG + 1):
            late = i - LAG
            n = late * V_BANKS
            largest(i - 1)
            exponentials(i - 1)
            products_pool(i, 0)
            products_vector(i, 0)
            if late >= 0:
                turned_for_vector(n + AHEAD)
            added_vector(n)
            terms_vector(n + 1)
            if late >= 0:
                turned_for_vector(n + 1 + AHEAD)
            terms_scalar(late, 0)
            weights(i - 1)
            terms_scalar(late, 1)
            finished(late - 1)
            products_pool(i, 1)
            products_vector(i, 1)
            added_vector(n + 1)
            if i == FIRST - 1:
                for k in range(FIRST, NCHUNK):
                    query_for_vector(k)
            terms_vector(n + 2)
            scores(i, 0)
            scores(i, 1)
            if 0 < i <= FIRST // 2:
                for k in range(FIRST + 2 * i - 2, FIRST + 2 * i):
                    looked_up(k)
                    rounded(k)
                    query_for_pool(k)
                    query_copied(k)
            if late >= 0:
                turned_for_vector(n + 2 + AHEAD)
            terms_vector(n + 3)
            turned_for_scalar(late + 1)
            added_vector(n + 2)
            added_scalar(late)
